import numpy as np
import ml_dtypes


def mxq(x, axis, fmt="e4m3"):
    dtype, down = {"e4m3": (ml_dtypes.float8_e4m3fn, 7), "e5m2": (ml_dtypes.float8_e5m2, 14)}[fmt]
    v = np.moveaxis(np.asarray(x, np.float32).astype(ml_dtypes.bfloat16).astype(np.float64), axis, -1)
    blocks = v.reshape(v.shape[:-1] + (-1, 32))
    amax = np.abs(blocks).max(-1, keepdims=True)
    byte = np.maximum(np.where(amax > 0, np.frexp(amax)[1] - 1 + 127, 0) - down, 1)
    scale = np.exp2(byte - 127.0)
    codes = (blocks / scale).astype(np.float32).astype(dtype).astype(np.float64)
    return np.moveaxis((codes * scale).reshape(v.shape), -1, axis)


WIDE = False


def mx_kscale(k):
    if not WIDE:
        return np.ones(k)
    levels = np.array([10, -10, 5, -5, 0])
    if k % 512:
        return np.exp2(np.random.permutation(np.resize(levels, k // 32))).repeat(32)
    a = np.empty((k // 512, 16))
    for p in range(k // 512):
        a[p, :8] = np.random.permutation(np.resize(levels, 8))
        for g in range(8):
            far = levels[np.abs(levels - a[p, g]) >= 10]
            a[p, g + 8] = far[np.random.randint(len(far))]
    return np.exp2(a.ravel()).repeat(32)


BF16 = ml_dtypes.bfloat16


def bf(x):
    return np.asarray(x, np.float32).astype(BF16)


def f64(x):
    return np.asarray(x).astype(np.float64)


B, S, D, A, H = 2, 512, 1024, 1024, 8
HD = A // H
ROTARY_BASE = 10000.0


def rotary_cos_sin():
    inv_freq = 1.0 / (ROTARY_BASE ** (np.arange(0, A, 2, dtype=np.float64) / A))
    t = np.arange(S, dtype=np.float64)
    freqs = t[:, None] * inv_freq[None, :]
    emb = np.concatenate([freqs, freqs], axis=-1)
    return np.cos(emb)[None], np.sin(emb)[None]


def rotate_half(x):
    x1, x2 = np.split(x, 2, axis=-1)
    return np.concatenate([-x2, x1], axis=-1)


def draw0():
    s = mx_kscale(D)
    return {"hidden_states": bf(np.random.standard_normal((B, S, D)) * s),
            "Wq": bf(np.random.standard_normal((A, D)) * 1.5 / np.sqrt(D) / s),
            "bq": bf(np.random.standard_normal(A) * 0.4),
            "Wk": bf(np.random.standard_normal((A, D)) * 0.5 / np.sqrt(D) / s),
            "bk": bf(np.random.standard_normal(A) * 0.15)}


def core(hidden_states, Wq, bq, Wk, bk):
    xq = mxq(f64(hidden_states), 2, "e4m3")
    q = (xq @ mxq(f64(Wq), 1, "e4m3").T) + f64(bq)
    k = (xq @ mxq(f64(Wk), 1, "e4m3").T) + f64(bk)
    q = q * (HD ** -0.5)
    cos, sin = rotary_cos_sin()
    q = q * cos + rotate_half(q) * sin
    k = k * cos + rotate_half(k) * sin
    return q, k


def e4m3fn_bytes(y):
    return np.clip(np.asarray(y, np.float64), -448.0, 448.0).astype(np.float32).astype(ml_dtypes.float8_e4m3fn).view(np.uint8)


def e4m3fn_values(b):
    return np.asarray(b, np.uint8).view(ml_dtypes.float8_e4m3fn).astype(np.float64)


def setup_inputs():
    d = draw0()
    x0 = np.asarray(d['hidden_states']).astype(np.float64)
    s = (np.max(np.abs(x0), axis=(0, 1), keepdims=True) / 448.0).astype(np.float32)
    out = {}
    for k, v in d.items():
        if k == 'hidden_states':
            out['hidden_states_bytes'] = e4m3fn_bytes(x0 / s.astype(np.float64))
            out['hidden_states_scale'] = s
        else:
            out[k] = v
    return out


def reference(hidden_states_bytes, hidden_states_scale, Wq, bq, Wk, bk):
    return core(e4m3fn_values(hidden_states_bytes) * hidden_states_scale.astype(np.float64), Wq, bq, Wk, bk)

@@ -1,0 +1,344 @@
+from contextlib import ExitStack
+
+import concourse.mybir as mybir
+from concourse.masks import make_identity
+
+FLOPS = 2 * 1024 * 1024 * 2048
+
+F32 = mybir.dt.float32
+BF16 = mybir.dt.bfloat16
+U8 = mybir.dt.uint8
+U32 = mybir.dt.uint32
+I32 = mybir.dt.int32
+FP8 = mybir.dt.float8_e4m3fn
+FP8X4 = mybir.dt.float8_e4m3fn_x4
+ALU = mybir.AluOpType
+ACTF = mybir.ActivationFunctionType
+
+P = 128
+S = 512
+D = 1024
+PI = 3.141592653589793
+RHO = 10000.0 ** (-1.0 / 512.0)
+QSCALE = 128.0 ** -0.5
+GWAY = ()
+PEADD = [(0, 1)] * 14 + [(1, 1), (1, 1)]
+NSIN_JB = (2, 3)
+WARM_EVERY = 2
+TOUT_BUFS = 4
+ORDER = list(range(16))
+KICK = 10
+FIRST_SLOT = 12
+SLOT_EVERY = 3
+
+
+def tile_sparseattention_pa_kernel(tc, x_bytes, x_scale, wq, bq, wk, bk, out_q, out_k):
+    nc = tc.nc
+    with ExitStack() as ctx:
+        const = ctx.enter_context(tc.tile_pool(name="const", bufs=1))
+        work = ctx.enter_context(tc.tile_pool(name="work", bufs=2))
+        psum = ctx.enter_context(tc.psum_pool(name="psum", bufs=4))
+        ctx.enter_context(tc.manual_schedule(engines={mybir.EngineType.PE}))
+
+        idle_rhs = const.tile([P, S], BF16, name="idle_rhs")
+        nc.vector.memset(idle_rhs[:], 0.0)
+
+        sc_bc = const.tile([P, D], F32, name="sc_bc")
+        nc.scalar.dma_start(out=sc_bc[:], in_=x_scale.rearrange("a b k -> (a b k)").partition_broadcast(P))
+        xb = []
+        for b in range(2):
+            xb_t = const.tile([P, 4 * D], U8, name="xbytes%d" % b)
+            xb.append(xb_t)
+        w_raw = {}
+        for w in range(8):
+            for h in range(2):
+                w_t = const.tile([P, D], BF16, name="wraw%d_%d" % (w, h))
+                w_raw[(w, h)] = w_t
+
+        seq = [("x", 0, 0), ("w", 0, 0), ("x", 0, 1), ("w", 0, 1), ("x", 0, 2), ("w", 1, 0), ("x", 0, 3), ("w", 1, 1),
+               ("w", 2, 0), ("w", 2, 1), ("x", 1, 0), ("w", 3, 0), ("x", 1, 1), ("w", 3, 1), ("x", 1, 2), ("w", 4, 0),
+               ("x", 1, 3), ("w", 4, 1)]
+        for w in (5, 6, 7):
+            seq.append(("w", w, 0))
+            seq.append(("w", w, 1))
+        for (kind, c0, c1) in seq:
+            if kind == "x":
+                nc.sync.dma_start(out=xb[c0][:, c1 * D:(c1 + 1) * D], in_=x_bytes[c0, c1 * P:(c1 + 1) * P, :])
+            else:
+                src = wq if c0 < 4 else wk
+                r0 = c1 * S + (c0 % 4) * P
+                nc.sync.dma_start(out=w_raw[(c0, c1)][:], in_=src[r0:r0 + P, :])
+
+        p_i = const.tile([P, 1], I32, name="p_i")
+        nc.gpsimd.iota(p_i[:], pattern=[[0, 1]], base=0, channel_multiplier=1)
+        ident_f = const.tile([P, P], F32, name="ident_f")
+        make_identity(nc, ident_f[:])
+        s_row = const.tile([P, S], F32, name="s_row")
+        nc.gpsimd.iota(s_row[:], pattern=[[1, S]], base=0, channel_multiplier=0,
+                       allow_small_or_imprecise_dtypes=True)
+        ident_b = const.tile([P, P], BF16, name="ident_b")
+        make_identity(nc, ident_b[:])
+        braw = const.tile([P, P], BF16, name="braw")
+        nc.vector.memset(braw[:], 0.0)
+        nc.gpsimd.dma_start(out=braw[0:8, :], in_=bq.rearrange("(m p) -> m p", p=P))
+        nc.gpsimd.dma_start(out=braw[8:16, :], in_=bk.rearrange("(m p) -> m p", p=P))
+
+        zero1 = const.tile([P, 1], F32, name="zero1")
+        nc.vector.memset(zero1[:], 0.0)
+        junk = const.tile([P, 1], F32, name="junk")
+        nc.scalar.activation(out=junk[:], in_=zero1[:], func=ACTF.Sin)
+
+        bits = const.tile([P, 8], I32, name="bits")
+        fac = const.tile([P, 8], F32, name="fac")
+        for k in range(7):
+            nc.vector.tensor_scalar(out=bits[:, k:k + 1], in0=p_i[:], scalar1=k, scalar2=1,
+                                    op0=ALU.logical_shift_right, op1=ALU.bitwise_and)
+        for k in range(7):
+            nc.vector.tensor_scalar(out=fac[:, k:k + 1], in0=bits[:, k:k + 1],
+                                    scalar1=RHO ** (2 ** k) - 1.0, scalar2=1.0,
+                                    op0=ALU.mult, op1=ALU.add)
+        nc.vector.tensor_scalar(out=fac[:, 7:8], in0=bits[:, 0:1], scalar1=0.0,
+                                scalar2=1.0 / (2.0 * PI), op0=ALU.mult, op1=ALU.add)
+        f4 = const.tile([P, 4], F32, name="f4")
+        nc.vector.tensor_tensor(out=f4[:], in0=fac[:, 0:4], in1=fac[:, 4:8], op=ALU.mult)
+        f2 = const.tile([P, 2], F32, name="f2")
+        nc.vector.tensor_tensor(out=f2[:], in0=f4[:, 0:2], in1=f4[:, 2:4], op=ALU.mult)
+        f1 = const.tile([P, 1], F32, name="f1")
+        nc.vector.tensor_tensor(out=f1[:], in0=f2[:, 0:1], in1=f2[:, 1:2], op=ALU.mult)
+        g4 = const.tile([P, 4], F32, name="g4")
+        for jb in range(4):
+            nc.vector.tensor_scalar(out=g4[:, jb:jb + 1], in0=f1[:], scalar1=RHO ** (128 * jb),
+                                    scalar2=None, op0=ALU.mult)
+
+        cos_t = const.tile([P, 4 * S], F32, name="cos_t")
+        sin_t = const.tile([P, 4 * S], F32, name="sin_t")
+        nsin_t = const.tile([P, 4 * S], F32, name="nsin_t")
+        d_all = const.tile([P, 4 * S], F32, name="d_all")
+
+        def table_turns(jb):
+            cols = slice(jb * S, (jb + 1) * S)
+            n_t = work.tile([P, S], I32, tag="n_t", name="n_t")
+            nc.gpsimd.tensor_scalar(out=n_t[:], in0=s_row[:], scalar1=g4[:, jb:jb + 1], scalar2=0.0,
+                                    op0=ALU.mult, op1=ALU.add)
+            nc.vector.scalar_tensor_tensor(out=d_all[:, cols], in0=s_row[:], scalar=g4[:, jb:jb + 1], in1=n_t[:],
+                                           op0=ALU.mult, op1=ALU.subtract)
+
+        def table_sincos(jb):
+            cols = slice(jb * S, (jb + 1) * S)
+            nc.scalar.activation(out=sin_t[:, cols], in_=d_all[:, cols], func=ACTF.Sin, scale=2.0 * PI)
+            a_t = work.tile([P, S], F32, tag="a_t", name="a_t")
+            nc.scalar.activation(out=a_t[:], in_=d_all[:, cols], func=ACTF.Abs)
+            nc.scalar.activation(out=cos_t[:, cols], in_=a_t[:], func=ACTF.Sin, scale=-2.0 * PI, bias=0.5 * PI)
+            if jb in NSIN_JB:
+                nc.scalar.activation(out=nsin_t[:, cols], in_=d_all[:, cols], func=ACTF.Sin, scale=-2.0 * PI)
+
+        bias = const.tile([P, 16], F32, name="bias")
+
+        def turn_bias():
+            bt_ps = psum.tile([P, P], BF16, tag="tout", bufs=TOUT_BUFS, name="bt_ps")
+            nc.tensor.transpose(bt_ps[:], braw[:], ident_b[:])
+            nc.vector.tensor_copy(out=bias[:], in_=bt_ps[:, 0:16])
+
+        xg, xcodes, xscales = [], [], []
+        for b in range(2):
+            xg_t = const.tile([P, 2 * S * 4], BF16, name="xg%d" % b, align_bytes=64)
+            xc_t = const.tile([P, 2 * S], U32, name="xcodes%d" % b, align_bytes=64)
+            xs_t = const.tile([P, 2 * S], U8, name="xscales%d" % b, align_bytes=64)
+            xg.append(xg_t)
+            xcodes.append(xc_t)
+            xscales.append(xs_t)
+        wcodes, wscales = [], []
+        for w in range(8):
+            wc_t = const.tile([P, 4 * P], U32, name="wcodes%d" % w, align_bytes=64)
+            ws_t = const.tile([P, 4 * P], U8, name="wscales%d" % w, align_bytes=64)
+            wcodes.append(wc_t)
+            wscales.append(ws_t)
+
+        turned = []
+
+        def turn(src_bf16):
+            words = src_bf16.bitcast(F32)
+            bank = psum.tile([P, 4 * P], F32, tag="tout", bufs=TOUT_BUFS, name="tin")
+            if len(turned) < FIRST_SLOT and len(turned) % WARM_EVERY == 0:
+                nc.tensor.matmul(out=bank[:], lhsT=idle_rhs[:, 0:P], rhs=idle_rhs[:], start=True, stop=True)
+            turned.append(1)
+            for g in range(2):
+                for u in range(2):
+                    c0 = (2 * g + u) * P
+                    nc.tensor.transpose(bank[:, c0:c0 + P], words[:, 256 * g + u:256 * (g + 1):2], ident_f[:])
+            return bank
+
+        xw_of = {}
+
+        def x_widen(b, a):
+            xw = work.tile([P, D], BF16, tag="xw", bufs=3, name="xw")
+            nc.vector.tensor_tensor(out=xw[:], in0=xb[b][:, a * D:(a + 1) * D].bitcast(FP8), in1=sc_bc[:], op=ALU.mult)
+            xw_of[(b, a)] = xw
+
+        def x_turn(b, a):
+            bank = turn(xw_of[(b, a)][:])
+            dst = xg[b][:].bitcast(F32).rearrange("p (g r u) -> p g r u", g=2, u=2)[:, :, a * P:(a + 1) * P, :]
+            nc.scalar.copy(out=dst, in_=bank[:].rearrange("p (g u r) -> p g r u", g=2, u=2))
+
+        def x_quant(b):
+            for g in range(2):
+                c0 = g * S
+                nc.vector.quantize_mx(out=xcodes[b][:, c0:c0 + S].bitcast(FP8X4), scales=xscales[b][:, c0:c0 + S],
+                                      in_=xg[b][:, 4 * c0:4 * (c0 + S)])
+
+        wg_of = {}
+
+        def w_turn(w, h):
+            if h == 0:
+                wg_new = work.tile([P, 2 * D], BF16, tag="wg", bufs=3, name="wg", align_bytes=64)
+                wg_of[w] = wg_new
+            bank = turn(w_raw[(w, h)][:])
+            nc.scalar.copy(out=wg_of[w][:, h * D:(h + 1) * D].bitcast(F32).rearrange("p (g r u) -> p g r u", g=2, u=2),
+                           in_=bank[:].rearrange("p (g u r) -> p g r u", g=2, u=2))
+
+        def w_quant(w):
+            nc.vector.quantize_mx(out=wcodes[w][:].bitcast(FP8X4), scales=wscales[w][:], in_=wg_of[w][:])
+
+        pairs = [(b, qk, jb) for b in range(2) for qk in range(2) for jb in range(4)]
+        acc_of = {}
+        prod_of = {}
+        sum_of = {}
+
+        def mx(i):
+            b, qk, jb = pairs[i]
+            w = qk * 4 + jb
+            accs = []
+            for h in range(2):
+                acc = psum.tile([P, S], F32, tag=("gacc" if i in GWAY else "acc"), bufs=(2 if i in GWAY else 4), name="acc")
+                for g in range(2):
+                    c0 = (2 * h + g) * P
+                    nc.tensor.matmul_mx(
+                        out=acc[:],
+                        lhsT=wcodes[w][:, c0:c0 + P].bitcast(FP8X4),
+                        lhsT_scale=wscales[w][:, c0:c0 + P],
+                        rhs=xcodes[b][:, g * S:(g + 1) * S].bitcast(FP8X4),
+                        rhs_scale=xscales[b][:, g * S:(g + 1) * S],
+                        start=(g == 0), stop=(g == 1),
+                    )
+                accs.append(acc)
+            acc_of[i] = accs
+
+        def pe_adds(i, h):
+            return PEADD[i][h] == 1
+
+        def products(i):
+            b, qk, jb = pairs[i]
+            cols = slice(jb * S, (jb + 1) * S)
+            minus = nsin_t if pe_adds(i, 0) else sin_t
+            bcol = [bias[:, qk * 8 + 4 * h + jb:qk * 8 + 4 * h + jb + 1] for h in range(2)]
+            ms = []
+            if i in GWAY:
+                moved = []
+                for h in range(2):
+                    mv = work.tile([P, S], F32, tag="mv%d" % h, bufs=2, name="mv%d" % h)
+                    nc.scalar.activation(out=mv[:], in_=acc_of[i][h][:], func=ACTF.Identity, bias=bcol[h])
+                    moved.append(mv)
+                for (nm, h, tab) in (("g1", 0, cos_t), ("g2", 1, minus), ("g3", 1, cos_t), ("g4m", 0, sin_t)):
+                    mt = work.tile([P, S], F32, tag=nm, bufs=2, name=nm)
+                    nc.gpsimd.tensor_tensor(out=mt[:], in0=moved[h][:], in1=tab[:, cols], op=ALU.mult)
+                    ms.append(mt)
+            else:
+                for (nm, h, tab) in (("m1", 0, cos_t), ("m2", 1, minus), ("m3", 1, cos_t), ("m4", 0, sin_t)):
+                    mt = work.tile([P, S], F32, tag=nm, bufs=4, name=nm)
+                    nc.vector.scalar_tensor_tensor(out=mt[:], in0=acc_of[i][h][:], scalar=bcol[h], in1=tab[:, cols],
+                                                   op0=ALU.add, op1=ALU.mult)
+                    ms.append(mt)
+            prod_of[i] = ms
+            res = {}
+            for h in range(2):
+                if not pe_adds(i, h):
+                    st = work.tile([P, S], F32, tag="sum%d" % h, bufs=3, name="sum%d" % h)
+                    nc.gpsimd.tensor_tensor(out=st[:], in0=ms[2 * h][:], in1=ms[2 * h + 1][:],
+                                            op=(ALU.subtract if h == 0 else ALU.add))
+                    res[h] = st
+            sum_of[i] = res
+
+        def finish(i, h):
+            b, qk, jb = pairs[i]
+            dram = (out_q if qk == 0 else out_k)[b].rearrange("(a p) j -> p a j", p=P)
+            bank = psum.tile([P, S], F32, tag="tout", bufs=TOUT_BUFS, name="tout")
+            for a in range(4):
+                blk = slice(a * P, (a + 1) * P)
+                if h in sum_of[i]:
+                    nc.tensor.transpose(bank[:, blk], sum_of[i][h][:, blk], ident_f[:])
+                else:
+                    nc.tensor.matmul(out=bank[:, blk], lhsT=prod_of[i][2 * h][:, blk], rhs=ident_f[:],
+                                     is_transpose=True, start=True, stop=False)
+                    nc.tensor.matmul(out=bank[:, blk], lhsT=prod_of[i][2 * h + 1][:, blk], rhs=ident_f[:],
+                                     is_transpose=True, start=False, stop=True)
+            ost = work.tile([P, S], F32, tag="ost", bufs=8, name="ost")
+            if qk == 0:
+                nc.scalar.activation(out=ost[:], in_=bank[:], func=ACTF.Copy, scale=QSCALE)
+            else:
+                nc.scalar.copy(out=ost[:], in_=bank[:])
+            j0 = h * S + jb * P
+            nc.sync.dma_start(out=dram[:, :, j0:j0 + P], in_=ost[:].rearrange("p (a j) -> p a j", a=4))
+
+        def quant(item):
+            if item[1] == "w":
+                w_quant(item[2])
+            else:
+                x_quant(item[2])
+
+        pending = []
+
+        def slot(k):
+            if k + 1 < 16:
+                mx(k + 1)
+            for item in list(pending):
+                if item[0] <= k:
+                    finish(item[1], item[2])
+                    pending.remove(item)
+            if k < 3:
+                table_sincos(k + 1)
+            products(k)
+            for h in range(2):
+                pending.append((k + 1 if pe_adds(k, h) else k + 2, k, h))
+
+        kick_ps = psum.tile([P, S], F32, tag="tout", bufs=TOUT_BUFS, name="kick_ps")
+        for n in range(KICK):
+            nc.tensor.matmul(out=kick_ps[:], lhsT=idle_rhs[:, 0:P], rhs=idle_rhs[:], start=True, stop=True)
+
+        x_widen(0, 0)
+        x_widen(0, 1)
+        due = []
+        slots_done = 0
+        for n in range(len(seq)):
+            kind, c0, c1 = seq[n]
+            if kind == "w":
+                w_turn(c0, c1)
+                if c1 == 1:
+                    due.append((n + 2, "w", c0))
+            else:
+                x_turn(c0, c1)
+                nxt = c0 * 4 + c1 + 2
+                if nxt < 8:
+                    x_widen(nxt // 4, nxt % 4)
+                if c1 == 3:
+                    due.append((n + 2, "x", c0))
+            for item in list(due):
+                if item[0] <= n:
+                    quant(item)
+                    due.remove(item)
+            if n in (1, 5, 9, 13):
+                table_turns((n - 1) // 4)
+            if n == 3:
+                table_sincos(0)
+            if n == 10:
+                turn_bias()
+            if n == FIRST_SLOT - 1:
+                mx(0)
+            if n >= FIRST_SLOT and (n - FIRST_SLOT) % SLOT_EVERY == 0:
+                slot(slots_done)
+                slots_done = slots_done + 1
+        for item in due:
+            quant(item)
+        for k in range(slots_done, 16):
+            slot(k)
+        for item in pending:
+            finish(item[1], item[2])

@@ -21,9 +21,7 @@ D = 1024
 PI = 3.141592653589793
 RHO = 10000.0 ** (-1.0 / 512.0)
 QSCALE = 128.0 ** -0.5
-GWAY = ()
 PEADD = [(0, 1)] * 14 + [(1, 1), (1, 1)]
-NSIN_JB = (2, 3)
 WARM_EVERY = 2
 TOUT_BUFS = 4
 ORDER = list(range(16))
@@ -110,9 +108,7 @@ def tile_sparseattention_pa_kernel(tc, x_bytes, x_scale, wq, bq, wk, bk, out_q, 
             nc.vector.tensor_scalar(out=g4[:, jb:jb + 1], in0=f1[:], scalar1=RHO ** (128 * jb),
                                     scalar2=None, op0=ALU.mult)
 
-        cos_t = const.tile([P, 4 * S], F32, name="cos_t")
-        sin_t = const.tile([P, 4 * S], F32, name="sin_t")
-        nsin_t = const.tile([P, 4 * S], F32, name="nsin_t")
+        tab = const.tile([P, 4, 3, S], F32, name="tab")
         d_all = const.tile([P, 4 * S], F32, name="d_all")
 
         def table_turns(jb):
@@ -125,12 +121,11 @@ def tile_sparseattention_pa_kernel(tc, x_bytes, x_scale, wq, bq, wk, bk, out_q, 
 
         def table_sincos(jb):
             cols = slice(jb * S, (jb + 1) * S)
-            nc.scalar.activation(out=sin_t[:, cols], in_=d_all[:, cols], func=ACTF.Sin, scale=2.0 * PI)
+            nc.scalar.activation(out=tab[:, jb, 2, :], in_=d_all[:, cols], func=ACTF.Sin, scale=2.0 * PI)
             a_t = work.tile([P, S], F32, tag="a_t", name="a_t")
             nc.scalar.activation(out=a_t[:], in_=d_all[:, cols], func=ACTF.Abs)
-            nc.scalar.activation(out=cos_t[:, cols], in_=a_t[:], func=ACTF.Sin, scale=-2.0 * PI, bias=0.5 * PI)
-            if jb in NSIN_JB:
-                nc.scalar.activation(out=nsin_t[:, cols], in_=d_all[:, cols], func=ACTF.Sin, scale=-2.0 * PI)
+            nc.scalar.activation(out=tab[:, jb, 1, :], in_=a_t[:], func=ACTF.Sin, scale=-2.0 * PI, bias=0.5 * PI)
+            nc.scalar.activation(out=tab[:, jb, 0, :], in_=d_all[:, cols], func=ACTF.Sin, scale=-2.0 * PI)
 
         bias = const.tile([P, 16], F32, name="bias")
 
@@ -209,7 +204,7 @@ def tile_sparseattention_pa_kernel(tc, x_bytes, x_scale, wq, bq, wk, bk, out_q, 
             w = qk * 4 + jb
             accs = []
             for h in range(2):
-                acc = psum.tile([P, S], F32, tag=("gacc" if i in GWAY else "acc"), bufs=(2 if i in GWAY else 4), name="acc")
+                acc = psum.tile([P, S], F32, tag="acc", bufs=4, name="acc")
                 for g in range(2):
                     c0 = (2 * h + g) * P
                     nc.tensor.matmul_mx(
@@ -228,33 +223,20 @@ def tile_sparseattention_pa_kernel(tc, x_bytes, x_scale, wq, bq, wk, bk, out_q, 
 
         def products(i):
             b, qk, jb = pairs[i]
-            cols = slice(jb * S, (jb + 1) * S)
-            minus = nsin_t if pe_adds(i, 0) else sin_t
-            bcol = [bias[:, qk * 8 + 4 * h + jb:qk * 8 + 4 * h + jb + 1] for h in range(2)]
-            ms = []
-            if i in GWAY:
-                moved = []
-                for h in range(2):
-                    mv = work.tile([P, S], F32, tag="mv%d" % h, bufs=2, name="mv%d" % h)
-                    nc.scalar.activation(out=mv[:], in_=acc_of[i][h][:], func=ACTF.Identity, bias=bcol[h])
-                    moved.append(mv)
-                for (nm, h, tab) in (("g1", 0, cos_t), ("g2", 1, minus), ("g3", 1, cos_t), ("g4m", 0, sin_t)):
-                    mt = work.tile([P, S], F32, tag=nm, bufs=2, name=nm)
-                    nc.gpsimd.tensor_tensor(out=mt[:], in0=moved[h][:], in1=tab[:, cols], op=ALU.mult)
-                    ms.append(mt)
-            else:
-                for (nm, h, tab) in (("m1", 0, cos_t), ("m2", 1, minus), ("m3", 1, cos_t), ("m4", 0, sin_t)):
-                    mt = work.tile([P, S], F32, tag=nm, bufs=4, name=nm)
-                    nc.vector.scalar_tensor_tensor(out=mt[:], in0=acc_of[i][h][:], scalar=bcol[h], in1=tab[:, cols],
-                                                   op0=ALU.add, op1=ALU.mult)
-                    ms.append(mt)
-            prod_of[i] = ms
+            m_lo = work.tile([P, 2, S], F32, tag="m_lo", bufs=4, name="m_lo")
+            m_hi = work.tile([P, 2, S], F32, tag="m_hi", bufs=4, name="m_hi")
+            for (h, mt, t0) in ((0, m_lo, 1), (1, m_hi, 0)):
+                c = qk * 8 + 4 * h + jb
+                nc.vector.scalar_tensor_tensor(out=mt[:], in0=acc_of[i][h][:].unsqueeze(1).to_broadcast([P, 2, S]),
+                                               scalar=bias[:, c:c + 1], in1=tab[:, jb, t0:t0 + 2, :],
+                                               op0=ALU.add, op1=ALU.mult)
+            prod_of[i] = [(m_lo, 0), (m_hi, 0), (m_hi, 1), (m_lo, 1)]
             res = {}
             for h in range(2):
                 if not pe_adds(i, h):
                     st = work.tile([P, S], F32, tag="sum%d" % h, bufs=3, name="sum%d" % h)
-                    nc.gpsimd.tensor_tensor(out=st[:], in0=ms[2 * h][:], in1=ms[2 * h + 1][:],
-                                            op=(ALU.subtract if h == 0 else ALU.add))
+                    (ta, ka), (tb, kb) = prod_of[i][2 * h], prod_of[i][2 * h + 1]
+                    nc.gpsimd.tensor_tensor(out=st[:], in0=ta[:, ka, :], in1=tb[:, kb, :], op=ALU.add)
                     res[h] = st
             sum_of[i] = res
 
@@ -267,9 +249,10 @@ def tile_sparseattention_pa_kernel(tc, x_bytes, x_scale, wq, bq, wk, bk, out_q, 
                 if h in sum_of[i]:
                     nc.tensor.transpose(bank[:, blk], sum_of[i][h][:, blk], ident_f[:])
                 else:
-                    nc.tensor.matmul(out=bank[:, blk], lhsT=prod_of[i][2 * h][:, blk], rhs=ident_f[:],
+                    (ta, ka), (tb, kb) = prod_of[i][2 * h], prod_of[i][2 * h + 1]
+                    nc.tensor.matmul(out=bank[:, blk], lhsT=ta[:, ka, blk], rhs=ident_f[:],
                                      is_transpose=True, start=True, stop=False)
-                    nc.tensor.matmul(out=bank[:, blk], lhsT=prod_of[i][2 * h + 1][:, blk], rhs=ident_f[:],
+                    nc.tensor.matmul(out=bank[:, blk], lhsT=tb[:, kb, blk], rhs=ident_f[:],
                                      is_transpose=True, start=False, stop=True)
             ost = work.tile([P, S], F32, tag="ost", bufs=8, name="ost")
             if qk == 0:

@@ -42,7 +42,7 @@ def tile_sparseattention_pa_kernel(tc, x_bytes, x_scale, wq, bq, wk, bk, out_q, 
         nc.vector.memset(idle_rhs[:], 0.0)
 
         sc_bc = const.tile([P, D], F32, name="sc_bc")
-        nc.scalar.dma_start(out=sc_bc[:], in_=x_scale.rearrange("a b k -> (a b k)").partition_broadcast(P))
+        nc.sync.dma_start(out=sc_bc[:], in_=x_scale.rearrange("a b k -> (a b k)").partition_broadcast(P))
         xb = []
         for b in range(2):
             xb_t = const.tile([P, 4 * D], U8, name="xbytes%d" % b)
@@ -104,12 +104,15 @@ def tile_sparseattention_pa_kernel(tc, x_bytes, x_scale, wq, bq, wk, bk, out_q, 
         f1 = const.tile([P, 1], F32, name="f1")
         nc.vector.tensor_tensor(out=f1[:], in0=f2[:, 0:1], in1=f2[:, 1:2], op=ALU.mult)
         g4 = const.tile([P, 4], F32, name="g4")
-        for jb in range(4):
+        for jb in range(3):
             nc.vector.tensor_scalar(out=g4[:, jb:jb + 1], in0=f1[:], scalar1=RHO ** (128 * jb),
                                     scalar2=None, op0=ALU.mult)
+        th3 = const.tile([P, 2], F32, name="th3")
+        nc.vector.tensor_scalar(out=th3[:, 0:1], in0=f1[:], scalar1=RHO ** 384 * 2.0 * PI, scalar2=None, op0=ALU.mult)
+        nc.vector.tensor_scalar(out=th3[:, 1:2], in0=f1[:], scalar1=-(RHO ** 384) * 2.0 * PI, scalar2=None, op0=ALU.mult)
 
         tab = const.tile([P, 4, 3, S], F32, name="tab")
-        d_all = const.tile([P, 4 * S], F32, name="d_all")
+        d_all = const.tile([P, 3 * S], F32, name="d_all")
 
         def table_turns(jb):
             cols = slice(jb * S, (jb + 1) * S)
@@ -120,6 +123,11 @@ def tile_sparseattention_pa_kernel(tc, x_bytes, x_scale, wq, bq, wk, bk, out_q, 
                                            op0=ALU.mult, op1=ALU.subtract)
 
         def table_sincos(jb):
+            if jb == 3:
+                nc.scalar.activation(out=tab[:, 3, 2, :], in_=s_row[:], func=ACTF.Sin, scale=th3[:, 0:1])
+                nc.scalar.activation(out=tab[:, 3, 1, :], in_=s_row[:], func=ACTF.Sin, scale=th3[:, 1:2], bias=0.5 * PI)
+                nc.scalar.activation(out=tab[:, 3, 0, :], in_=s_row[:], func=ACTF.Sin, scale=th3[:, 1:2])
+                return
             cols = slice(jb * S, (jb + 1) * S)
             nc.scalar.activation(out=tab[:, jb, 2, :], in_=d_all[:, cols], func=ACTF.Sin, scale=2.0 * PI)
             a_t = work.tile([P, S], F32, tag="a_t", name="a_t")
@@ -176,10 +184,7 @@ def tile_sparseattention_pa_kernel(tc, x_bytes, x_scale, wq, bq, wk, bk, out_q, 
             nc.scalar.copy(out=dst, in_=bank[:].rearrange("p (g u r) -> p g r u", g=2, u=2))
 
         def x_quant(b):
-            for g in range(2):
-                c0 = g * S
-                nc.vector.quantize_mx(out=xcodes[b][:, c0:c0 + S].bitcast(FP8X4), scales=xscales[b][:, c0:c0 + S],
-                                      in_=xg[b][:, 4 * c0:4 * (c0 + S)])
+            nc.vector.quantize_mx(out=xcodes[b][:].bitcast(FP8X4), scales=xscales[b][:], in_=xg[b][:])
 
         wg_of = {}
 
@@ -308,7 +313,7 @@ def tile_sparseattention_pa_kernel(tc, x_bytes, x_scale, wq, bq, wk, bk, out_q, 
                 if item[0] <= n:
                     quant(item)
                     due.remove(item)
-            if n in (1, 5, 9, 13):
+            if n in (1, 5, 9):
                 table_turns((n - 1) // 4)
             if n == 3:
                 table_sincos(0)

@@ -21,7 +21,7 @@ D = 1024
 PI = 3.141592653589793
 RHO = 10000.0 ** (-1.0 / 512.0)
 QSCALE = 128.0 ** -0.5
-PEADD = [(0, 1)] * 14 + [(1, 1), (1, 1)]
+PEADD = [(0, 1)] * 15 + [(2, 2)]
 WARM_EVERY = 2
 TOUT_BUFS = 4
 ORDER = list(range(16))
@@ -104,15 +104,18 @@ def tile_sparseattention_pa_kernel(tc, x_bytes, x_scale, wq, bq, wk, bk, out_q, 
         f1 = const.tile([P, 1], F32, name="f1")
         nc.vector.tensor_tensor(out=f1[:], in0=f2[:, 0:1], in1=f2[:, 1:2], op=ALU.mult)
         g4 = const.tile([P, 4], F32, name="g4")
-        for jb in range(3):
+        for jb in range(2):
             nc.vector.tensor_scalar(out=g4[:, jb:jb + 1], in0=f1[:], scalar1=RHO ** (128 * jb),
                                     scalar2=None, op0=ALU.mult)
+        th2 = const.tile([P, 2], F32, name="th2")
+        nc.vector.tensor_scalar(out=th2[:, 0:1], in0=f1[:], scalar1=RHO ** 256 * 2.0 * PI, scalar2=None, op0=ALU.mult)
+        nc.vector.tensor_scalar(out=th2[:, 1:2], in0=f1[:], scalar1=-(RHO ** 256) * 2.0 * PI, scalar2=None, op0=ALU.mult)
         th3 = const.tile([P, 2], F32, name="th3")
         nc.vector.tensor_scalar(out=th3[:, 0:1], in0=f1[:], scalar1=RHO ** 384 * 2.0 * PI, scalar2=None, op0=ALU.mult)
         nc.vector.tensor_scalar(out=th3[:, 1:2], in0=f1[:], scalar1=-(RHO ** 384) * 2.0 * PI, scalar2=None, op0=ALU.mult)
 
         tab = const.tile([P, 4, 3, S], F32, name="tab")
-        d_all = const.tile([P, 3 * S], F32, name="d_all")
+        d_all = const.tile([P, 2 * S], F32, name="d_all")
 
         def table_turns(jb):
             cols = slice(jb * S, (jb + 1) * S)
@@ -127,6 +130,19 @@ def tile_sparseattention_pa_kernel(tc, x_bytes, x_scale, wq, bq, wk, bk, out_q, 
                 nc.scalar.activation(out=tab[:, 3, 2, :], in_=s_row[:], func=ACTF.Sin, scale=th3[:, 0:1])
                 nc.scalar.activation(out=tab[:, 3, 1, :], in_=s_row[:], func=ACTF.Sin, scale=th3[:, 1:2], bias=0.5 * PI)
                 nc.scalar.activation(out=tab[:, 3, 0, :], in_=s_row[:], func=ACTF.Sin, scale=th3[:, 1:2])
+                return
+            if jb == 2:
+                fh = slice(0, S // 2)
+                sh = slice(S // 2, S)
+                plus, minus = th2[:, 0:1], th2[:, 1:2]
+                nc.scalar.activation(out=tab[:, 2, 2, fh], in_=s_row[:, fh], func=ACTF.Sin, scale=plus)
+                nc.scalar.activation(out=tab[:, 2, 2, sh], in_=s_row[:, sh], func=ACTF.Sin, scale=minus, bias=PI)
+                nc.scalar.activation(out=tab[:, 2, 1, fh], in_=s_row[:, fh], func=ACTF.Sin, scale=minus, bias=0.5 * PI)
+                a_h = work.tile([P, S // 2], F32, tag="a_h", name="a_h")
+                nc.scalar.activation(out=a_h[:], in_=s_row[:, sh], func=ACTF.Abs, scale=plus, bias=-PI)
+                nc.scalar.activation(out=tab[:, 2, 1, sh], in_=a_h[:], func=ACTF.Sin, bias=-0.5 * PI)
+                nc.scalar.activation(out=tab[:, 2, 0, fh], in_=s_row[:, fh], func=ACTF.Sin, scale=minus)
+                nc.scalar.activation(out=tab[:, 2, 0, sh], in_=s_row[:, sh], func=ACTF.Sin, scale=plus, bias=-PI)
                 return
             cols = slice(jb * S, (jb + 1) * S)
             nc.scalar.activation(out=tab[:, jb, 2, :], in_=d_all[:, cols], func=ACTF.Sin, scale=2.0 * PI)
@@ -241,7 +257,8 @@ def tile_sparseattention_pa_kernel(tc, x_bytes, x_scale, wq, bq, wk, bk, out_q, 
                 if not pe_adds(i, h):
                     st = work.tile([P, S], F32, tag="sum%d" % h, bufs=3, name="sum%d" % h)
                     (ta, ka), (tb, kb) = prod_of[i][2 * h], prod_of[i][2 * h + 1]
-                    nc.gpsimd.tensor_tensor(out=st[:], in0=ta[:, ka, :], in1=tb[:, kb, :], op=ALU.add)
+                    adder = nc.vector if PEADD[i][h] == 2 else nc.gpsimd
+                    adder.tensor_tensor(out=st[:], in0=ta[:, ka, :], in1=tb[:, kb, :], op=ALU.add)
                     res[h] = st
             sum_of[i] = res
 
@@ -286,7 +303,7 @@ def tile_sparseattention_pa_kernel(tc, x_bytes, x_scale, wq, bq, wk, bk, out_q, 
                 table_sincos(k + 1)
             products(k)
             for h in range(2):
-                pending.append((k + 1 if pe_adds(k, h) else k + 2, k, h))
+                pending.append((k + 2 if PEADD[k][h] == 0 else k + 1, k, h))
 
         kick_ps = psum.tile([P, S], F32, tag="tout", bufs=TOUT_BUFS, name="kick_ps")
         for n in range(KICK):
@@ -313,7 +330,7 @@ def tile_sparseattention_pa_kernel(tc, x_bytes, x_scale, wq, bq, wk, bk, out_q, 
                 if item[0] <= n:
                     quant(item)
                     due.remove(item)
-            if n in (1, 5, 9):
+            if n in (1, 5):
                 table_turns((n - 1) // 4)
             if n == 3:
                 table_sincos(0)

@@ -114,7 +114,7 @@ def tile_sparseattention_pa_kernel(tc, x_bytes, x_scale, wq, bq, wk, bk, out_q, 
         nc.vector.tensor_scalar(out=th3[:, 0:1], in0=f1[:], scalar1=RHO ** 384 * 2.0 * PI, scalar2=None, op0=ALU.mult)
         nc.vector.tensor_scalar(out=th3[:, 1:2], in0=f1[:], scalar1=-(RHO ** 384) * 2.0 * PI, scalar2=None, op0=ALU.mult)
 
-        tab = const.tile([P, 4, 3, S], F32, name="tab")
+        tab = const.tile([P, 4, 2, S], F32, name="tab")
         d_all = const.tile([P, 2 * S], F32, name="d_all")
 
         def table_turns(jb):
@@ -127,29 +127,25 @@ def tile_sparseattention_pa_kernel(tc, x_bytes, x_scale, wq, bq, wk, bk, out_q, 
 
         def table_sincos(jb):
             if jb == 3:
-                nc.scalar.activation(out=tab[:, 3, 2, :], in_=s_row[:], func=ACTF.Sin, scale=th3[:, 0:1])
-                nc.scalar.activation(out=tab[:, 3, 1, :], in_=s_row[:], func=ACTF.Sin, scale=th3[:, 1:2], bias=0.5 * PI)
-                nc.scalar.activation(out=tab[:, 3, 0, :], in_=s_row[:], func=ACTF.Sin, scale=th3[:, 1:2])
+                nc.scalar.activation(out=tab[:, 3, 1, :], in_=s_row[:], func=ACTF.Sin, scale=th3[:, 0:1])
+                nc.scalar.activation(out=tab[:, 3, 0, :], in_=s_row[:], func=ACTF.Sin, scale=th3[:, 1:2], bias=0.5 * PI)
                 return
             if jb == 2:
                 fh = slice(0, S // 2)
                 sh = slice(S // 2, S)
                 plus, minus = th2[:, 0:1], th2[:, 1:2]
-                nc.scalar.activation(out=tab[:, 2, 2, fh], in_=s_row[:, fh], func=ACTF.Sin, scale=plus)
-                nc.scalar.activation(out=tab[:, 2, 2, sh], in_=s_row[:, sh], func=ACTF.Sin, scale=minus, bias=PI)
-                nc.scalar.activation(out=tab[:, 2, 1, fh], in_=s_row[:, fh], func=ACTF.Sin, scale=minus, bias=0.5 * PI)
+                nc.scalar.activation(out=tab[:, 2, 1, fh], in_=s_row[:, fh], func=ACTF.Sin, scale=plus)
+                nc.scalar.activation(out=tab[:, 2, 1, sh], in_=s_row[:, sh], func=ACTF.Sin, scale=minus, bias=PI)
+                nc.scalar.activation(out=tab[:, 2, 0, fh], in_=s_row[:, fh], func=ACTF.Sin, scale=minus, bias=0.5 * PI)
                 a_h = work.tile([P, S // 2], F32, tag="a_h", name="a_h")
                 nc.scalar.activation(out=a_h[:], in_=s_row[:, sh], func=ACTF.Abs, scale=plus, bias=-PI)
-                nc.scalar.activation(out=tab[:, 2, 1, sh], in_=a_h[:], func=ACTF.Sin, bias=-0.5 * PI)
-                nc.scalar.activation(out=tab[:, 2, 0, fh], in_=s_row[:, fh], func=ACTF.Sin, scale=minus)
-                nc.scalar.activation(out=tab[:, 2, 0, sh], in_=s_row[:, sh], func=ACTF.Sin, scale=plus, bias=-PI)
+                nc.scalar.activation(out=tab[:, 2, 0, sh], in_=a_h[:], func=ACTF.Sin, bias=-0.5 * PI)
                 return
             cols = slice(jb * S, (jb + 1) * S)
-            nc.scalar.activation(out=tab[:, jb, 2, :], in_=d_all[:, cols], func=ACTF.Sin, scale=2.0 * PI)
+            nc.scalar.activation(out=tab[:, jb, 1, :], in_=d_all[:, cols], func=ACTF.Sin, scale=2.0 * PI)
             a_t = work.tile([P, S], F32, tag="a_t", name="a_t")
             nc.scalar.activation(out=a_t[:], in_=d_all[:, cols], func=ACTF.Abs)
-            nc.scalar.activation(out=tab[:, jb, 1, :], in_=a_t[:], func=ACTF.Sin, scale=-2.0 * PI, bias=0.5 * PI)
-            nc.scalar.activation(out=tab[:, jb, 0, :], in_=d_all[:, cols], func=ACTF.Sin, scale=-2.0 * PI)
+            nc.scalar.activation(out=tab[:, jb, 0, :], in_=a_t[:], func=ACTF.Sin, scale=-2.0 * PI, bias=0.5 * PI)
 
         bias = const.tile([P, 16], F32, name="bias")
 
@@ -246,19 +242,19 @@ def tile_sparseattention_pa_kernel(tc, x_bytes, x_scale, wq, bq, wk, bk, out_q, 
             b, qk, jb = pairs[i]
             m_lo = work.tile([P, 2, S], F32, tag="m_lo", bufs=4, name="m_lo")
             m_hi = work.tile([P, 2, S], F32, tag="m_hi", bufs=4, name="m_hi")
-            for (h, mt, t0) in ((0, m_lo, 1), (1, m_hi, 0)):
+            for (h, mt) in ((0, m_lo), (1, m_hi)):
                 c = qk * 8 + 4 * h + jb
                 nc.vector.scalar_tensor_tensor(out=mt[:], in0=acc_of[i][h][:].unsqueeze(1).to_broadcast([P, 2, S]),
-                                               scalar=bias[:, c:c + 1], in1=tab[:, jb, t0:t0 + 2, :],
+                                               scalar=bias[:, c:c + 1], in1=tab[:, jb, :, :],
                                                op0=ALU.add, op1=ALU.mult)
-            prod_of[i] = [(m_lo, 0), (m_hi, 0), (m_hi, 1), (m_lo, 1)]
+            prod_of[i] = [(m_lo, 0), (m_hi, 1), (m_hi, 0), (m_lo, 1)]
             res = {}
             for h in range(2):
                 if not pe_adds(i, h):
                     st = work.tile([P, S], F32, tag="sum%d" % h, bufs=3, name="sum%d" % h)
                     (ta, ka), (tb, kb) = prod_of[i][2 * h], prod_of[i][2 * h + 1]
                     adder = nc.vector if PEADD[i][h] == 2 else nc.gpsimd
-                    adder.tensor_tensor(out=st[:], in0=ta[:, ka, :], in1=tb[:, kb, :], op=ALU.add)
+                    adder.tensor_tensor(out=st[:], in0=ta[:, ka, :], in1=tb[:, kb, :], op=(ALU.subtract if h == 0 else ALU.add))
                     res[h] = st
             sum_of[i] = res
 

@@ -25,7 +25,8 @@ PEADD = [(0, 1)] * 15 + [(2, 2)]
 WARM_EVERY = 2
 TOUT_BUFS = 4
 ORDER = list(range(16))
-KICK = 10
+KICK = 5
+CH = 256
 FIRST_SLOT = 12
 SLOT_EVERY = 3
 
@@ -40,9 +41,13 @@ def tile_sparseattention_pa_kernel(tc, x_bytes, x_scale, wq, bq, wk, bk, out_q, 
 
         idle_rhs = const.tile([P, S], BF16, name="idle_rhs")
         nc.vector.memset(idle_rhs[:], 0.0)
+        zrow = const.tile([P, D], F32, name="zrow")
+        nc.vector.memset(zrow[:], 0.0)
+        ones_f = const.tile([P, P], F32, name="ones_f")
+        nc.vector.memset(ones_f[:], 1.0)
 
         sc_bc = const.tile([P, D], F32, name="sc_bc")
-        nc.sync.dma_start(out=sc_bc[:], in_=x_scale.rearrange("a b k -> (a b k)").partition_broadcast(P))
+        nc.sync.dma_start(out=zrow[0:1, :], in_=x_scale.rearrange("a b k -> (a b) k"))
         xb = []
         for b in range(2):
             xb_t = const.tile([P, 4 * D], U8, name="xbytes%d" % b)
@@ -187,7 +192,10 @@ def tile_sparseattention_pa_kernel(tc, x_bytes, x_scale, wq, bq, wk, bk, out_q, 
 
         def x_widen(b, a):
             xw = work.tile([P, D], BF16, tag="xw", bufs=3, name="xw")
-            nc.vector.tensor_tensor(out=xw[:], in0=xb[b][:, a * D:(a + 1) * D].bitcast(FP8), in1=sc_bc[:], op=ALU.mult)
+            wd = CH if (b, a) == (0, 0) else D
+            for c0 in range(0, D, wd):
+                nc.vector.tensor_tensor(out=xw[:, c0:c0 + wd], in0=xb[b][:, a * D + c0:a * D + c0 + wd].bitcast(FP8),
+                                        in1=sc_bc[:, c0:c0 + wd], op=ALU.mult)
             xw_of[(b, a)] = xw
 
         def x_turn(b, a):
@@ -305,6 +313,10 @@ def tile_sparseattention_pa_kernel(tc, x_bytes, x_scale, wq, bq, wk, bk, out_q, 
         for n in range(KICK):
             nc.tensor.matmul(out=kick_ps[:], lhsT=idle_rhs[:, 0:P], rhs=idle_rhs[:], start=True, stop=True)
 
+        for c0 in range(0, D, CH):
+            sc_ps = psum.tile([P, CH], F32, tag="tout", bufs=TOUT_BUFS, name="sc_ps")
+            nc.tensor.matmul(out=sc_ps[:], lhsT=ones_f[:], rhs=zrow[:, c0:c0 + CH], start=True, stop=True)
+            nc.scalar.copy(out=sc_bc[:, c0:c0 + CH], in_=sc_ps[:])
         x_widen(0, 0)
         x_widen(0, 1)
         due = []

@@ -22,7 +22,6 @@ PI = 3.141592653589793
 RHO = 10000.0 ** (-1.0 / 512.0)
 QSCALE = 128.0 ** -0.5
 PEADD = [(0, 1)] * 15 + [(2, 2)]
-WARM_EVERY = 2
 TOUT_BUFS = 4
 ORDER = list(range(16))
 KICK = 5
@@ -174,14 +173,9 @@ def tile_sparseattention_pa_kernel(tc, x_bytes, x_scale, wq, bq, wk, bk, out_q, 
             wcodes.append(wc_t)
             wscales.append(ws_t)
 
-        turned = []
-
         def turn(src_bf16):
             words = src_bf16.bitcast(F32)
             bank = psum.tile([P, 4 * P], F32, tag="tout", bufs=TOUT_BUFS, name="tin")
-            if len(turned) < FIRST_SLOT and len(turned) % WARM_EVERY == 0:
-                nc.tensor.matmul(out=bank[:], lhsT=idle_rhs[:, 0:P], rhs=idle_rhs[:], start=True, stop=True)
-            turned.append(1)
             for g in range(2):
                 for u in range(2):
                     c0 = (2 * g + u) * P

@@ -40,13 +40,11 @@ def tile_sparseattention_pa_kernel(tc, x_bytes, x_scale, wq, bq, wk, bk, out_q, 
 
         idle_rhs = const.tile([P, S], BF16, name="idle_rhs")
         nc.vector.memset(idle_rhs[:], 0.0)
-        zrow = const.tile([P, D], F32, name="zrow")
+        zrow = const.tile([P, P], F32, name="zrow")
         nc.vector.memset(zrow[:], 0.0)
-        ones_f = const.tile([P, P], F32, name="ones_f")
-        nc.vector.memset(ones_f[:], 1.0)
 
         sc_bc = const.tile([P, D], F32, name="sc_bc")
-        nc.sync.dma_start(out=zrow[0:1, :], in_=x_scale.rearrange("a b k -> (a b) k"))
+        nc.sync.dma_start(out=zrow[0:8, :], in_=x_scale.rearrange("a b (c p) -> (a b c) p", p=P))
         xb = []
         for b in range(2):
             xb_t = const.tile([P, 4 * D], U8, name="xbytes%d" % b)
@@ -307,9 +305,15 @@ def tile_sparseattention_pa_kernel(tc, x_bytes, x_scale, wq, bq, wk, bk, out_q, 
         for n in range(KICK):
             nc.tensor.matmul(out=kick_ps[:], lhsT=idle_rhs[:, 0:P], rhs=idle_rhs[:], start=True, stop=True)
 
+        sv_ps = psum.tile([P, P], F32, tag="tout", bufs=TOUT_BUFS, name="sv_ps")
+        nc.tensor.transpose(sv_ps[:], zrow[:], ident_f[:])
+        sv = const.tile([P, 8], F32, name="sv")
+        nc.vector.tensor_copy(out=sv[:], in_=sv_ps[:, 0:8])
         for c0 in range(0, D, CH):
             sc_ps = psum.tile([P, CH], F32, tag="tout", bufs=TOUT_BUFS, name="sc_ps")
-            nc.tensor.matmul(out=sc_ps[:], lhsT=ones_f[:], rhs=zrow[:, c0:c0 + CH], start=True, stop=True)
+            for c in range(CH // P):
+                col = c0 // P + c
+                nc.tensor.transpose(sc_ps[:, c * P:(c + 1) * P], sv[:, col:col + 1].to_broadcast([P, P]), ident_f[:])
             nc.scalar.copy(out=sc_bc[:, c0:c0 + CH], in_=sc_ps[:])
         x_widen(0, 0)
         x_widen(0, 1)

@@ -328,16 +328,18 @@ def tile_sparseattention_pa_kernel(tc, x_bytes, x_scale, wq, bq, wk, bk, out_q, 
             else:
                 x_turn(c0, c1)
                 nxt = c0 * 4 + c1 + 2
-                if nxt < 8:
+                if nxt < 8 and nxt != 5:
                     x_widen(nxt // 4, nxt % 4)
                 if c1 == 3:
-                    due.append((n + 2, "x", c0))
+                    due.append((n + 1, "x", c0))
             for item in list(due):
                 if item[0] <= n:
                     quant(item)
                     due.remove(item)
-            if n in (1, 5):
-                table_turns((n - 1) // 4)
+            if n == 7:
+                x_widen(1, 1)
+            if n in (1, 9):
+                table_turns((n - 1) // 8)
             if n == 3:
                 table_sincos(0)
             if n == 10:

@@ -28,6 +28,7 @@ KICK = 5
 CH = 256
 FIRST_SLOT = 12
 SLOT_EVERY = 3
+WORD = [0, 4, 1, 5, 2, 6, 3, 7]
 
 
 def tile_sparseattention_pa_kernel(tc, x_bytes, x_scale, wq, bq, wk, bk, out_q, out_k):
@@ -61,6 +62,7 @@ def tile_sparseattention_pa_kernel(tc, x_bytes, x_scale, wq, bq, wk, bk, out_q, 
         for w in (5, 6, 7):
             seq.append(("w", w, 0))
             seq.append(("w", w, 1))
+        seq = [(kind, (WORD[c0] if kind == "w" else c0), c1) for (kind, c0, c1) in seq]
         for (kind, c0, c1) in seq:
             if kind == "x":
                 nc.sync.dma_start(out=xb[c0][:, c1 * D:(c1 + 1) * D], in_=x_bytes[c0, c1 * P:(c1 + 1) * P, :])
@@ -211,7 +213,7 @@ def tile_sparseattention_pa_kernel(tc, x_bytes, x_scale, wq, bq, wk, bk, out_q, 
         def w_quant(w):
             nc.vector.quantize_mx(out=wcodes[w][:].bitcast(FP8X4), scales=wscales[w][:], in_=wg_of[w][:])
 
-        pairs = [(b, qk, jb) for b in range(2) for qk in range(2) for jb in range(4)]
+        pairs = [(b, qk, jb) for b in range(2) for jb in range(4) for qk in range(2)]
         acc_of = {}
         prod_of = {}
         sum_of = {}
@@ -295,8 +297,8 @@ def tile_sparseattention_pa_kernel(tc, x_bytes, x_scale, wq, bq, wk, bk, out_q, 
                 if item[0] <= k:
                     finish(item[1], item[2])
                     pending.remove(item)
-            if k < 3:
-                table_sincos(k + 1)
+            if k in (1, 3, 5):
+                table_sincos((k + 1) // 2)
             products(k)
             for h in range(2):
                 pending.append((k + 2 if PEADD[k][h] == 0 else k + 1, k, h))

@@ -124,10 +124,13 @@ def tile_sparseattention_pa_kernel(tc, x_bytes, x_scale, wq, bq, wk, bk, out_q, 
         def table_turns(jb):
             cols = slice(jb * S, (jb + 1) * S)
             n_t = work.tile([P, S], I32, tag="n_t", name="n_t")
-            nc.gpsimd.tensor_scalar(out=n_t[:], in0=s_row[:], scalar1=g4[:, jb:jb + 1], scalar2=0.0,
+            nc.vector.tensor_scalar(out=n_t[:], in0=s_row[:], scalar1=g4[:, jb:jb + 1], scalar2=0.0,
                                     op0=ALU.mult, op1=ALU.add)
             nc.vector.scalar_tensor_tensor(out=d_all[:, cols], in0=s_row[:], scalar=g4[:, jb:jb + 1], in1=n_t[:],
                                            op0=ALU.mult, op1=ALU.subtract)
+
+        table_turns(0)
+        table_turns(1)
 
         def table_sincos(jb):
             if jb == 3:
@@ -310,7 +313,7 @@ def tile_sparseattention_pa_kernel(tc, x_bytes, x_scale, wq, bq, wk, bk, out_q, 
         sv_ps = psum.tile([P, P], F32, tag="tout", bufs=TOUT_BUFS, name="sv_ps")
         nc.tensor.transpose(sv_ps[:], zrow[:], ident_f[:])
         sv = const.tile([P, 8], F32, name="sv")
-        nc.vector.tensor_copy(out=sv[:], in_=sv_ps[:, 0:8])
+        nc.scalar.copy(out=sv[:], in_=sv_ps[:, 0:8])
         for c0 in range(0, D, CH):
             sc_ps = psum.tile([P, CH], F32, tag="tout", bufs=TOUT_BUFS, name="sc_ps")
             for c in range(CH // P):
@@ -340,8 +343,6 @@ def tile_sparseattention_pa_kernel(tc, x_bytes, x_scale, wq, bq, wk, bk, out_q, 
                     due.remove(item)
             if n == 7:
                 x_widen(1, 1)
-            if n in (1, 9):
-                table_turns((n - 1) // 8)
             if n == 3:
                 table_sincos(0)
             if n == 10:

@@ -29,6 +29,7 @@ CH = 256
 FIRST_SLOT = 12
 SLOT_EVERY = 3
 WORD = [0, 4, 1, 5, 2, 6, 3, 7]
+SHORT_SUMS = 4
 
 
 def tile_sparseattention_pa_kernel(tc, x_bytes, x_scale, wq, bq, wk, bk, out_q, out_k):
@@ -259,7 +260,10 @@ def tile_sparseattention_pa_kernel(tc, x_bytes, x_scale, wq, bq, wk, bk, out_q, 
                     st = work.tile([P, S], F32, tag="sum%d" % h, bufs=3, name="sum%d" % h)
                     (ta, ka), (tb, kb) = prod_of[i][2 * h], prod_of[i][2 * h + 1]
                     adder = nc.vector if PEADD[i][h] == 2 else nc.gpsimd
-                    adder.tensor_tensor(out=st[:], in0=ta[:, ka, :], in1=tb[:, kb, :], op=(ALU.subtract if h == 0 else ALU.add))
+                    wd = P if (PEADD[i][h] == 0 and i < SHORT_SUMS) else S
+                    for c0 in range(0, S, wd):
+                        adder.tensor_tensor(out=st[:, c0:c0 + wd], in0=ta[:, ka, c0:c0 + wd], in1=tb[:, kb, c0:c0 + wd],
+                                            op=(ALU.subtract if h == 0 else ALU.add))
                     res[h] = st
             sum_of[i] = res
 

@@ -30,6 +30,8 @@ FIRST_SLOT = 12
 SLOT_EVERY = 3
 WORD = [0, 4, 1, 5, 2, 6, 3, 7]
 SHORT_SUMS = 4
+GP = 3
+GP_SLOTS = [4, 6, 8, 10, 12]
 
 
 def tile_sparseattention_pa_kernel(tc, x_bytes, x_scale, wq, bq, wk, bk, out_q, out_k):
@@ -38,7 +40,7 @@ def tile_sparseattention_pa_kernel(tc, x_bytes, x_scale, wq, bq, wk, bk, out_q, 
         const = ctx.enter_context(tc.tile_pool(name="const", bufs=1))
         work = ctx.enter_context(tc.tile_pool(name="work", bufs=2))
         psum = ctx.enter_context(tc.psum_pool(name="psum", bufs=4))
-        ctx.enter_context(tc.manual_schedule(engines={mybir.EngineType.PE}))
+        ctx.enter_context(tc.manual_schedule(engines={mybir.EngineType.PE, mybir.EngineType.Pool}))
 
         idle_rhs = const.tile([P, S], BF16, name="idle_rhs")
         nc.vector.memset(idle_rhs[:], 0.0)
@@ -267,6 +269,38 @@ def tile_sparseattention_pa_kernel(tc, x_bytes, x_scale, wq, bq, wk, bk, out_q, 
                     res[h] = st
             sum_of[i] = res
 
+        gp_tiles = {}
+
+        def gp_evac():
+            b, qk, jb = pairs[GP]
+            for h in range(2):
+                ev = const.tile([P, S], F32, name="gp_ev%d" % h)
+                c = qk * 8 + 4 * h + jb
+                nc.scalar.activation(out=ev[:], in_=acc_of[GP][h][:], func=ACTF.Identity, bias=bias[:, c:c + 1])
+                gp_tiles["ev%d" % h] = ev
+            g_lo = const.tile([P, 2, S], F32, name="gp_lo")
+            g_hi = const.tile([P, 2, S], F32, name="gp_hi")
+            g_st = const.tile([P, S], F32, name="gp_st")
+            gp_tiles["lo"] = g_lo
+            gp_tiles["hi"] = g_hi
+            prod_of[GP] = [(g_lo, 0), (g_lo, 1), (g_hi, 0), (g_hi, 1)]
+            sum_of[GP] = {0: g_st}
+
+        def gp_step(n):
+            b, qk, jb = pairs[GP]
+            ev_lo, ev_hi = gp_tiles["ev0"], gp_tiles["ev1"]
+            g_lo, g_hi = gp_tiles["lo"], gp_tiles["hi"]
+            if n == 0:
+                nc.gpsimd.tensor_tensor(out=g_lo[:, 0, :], in0=ev_lo[:], in1=tab[:, jb, 0, :], op=ALU.mult)
+            if n == 1:
+                nc.gpsimd.tensor_tensor(out=g_lo[:, 1, :], in0=ev_hi[:], in1=tab[:, jb, 1, :], op=ALU.mult)
+            if n == 2:
+                nc.gpsimd.tensor_tensor(out=sum_of[GP][0][:], in0=g_lo[:, 0, :], in1=g_lo[:, 1, :], op=ALU.subtract)
+            if n == 3:
+                nc.gpsimd.tensor_tensor(out=g_hi[:, 0, :], in0=ev_hi[:], in1=tab[:, jb, 0, :], op=ALU.mult)
+            if n == 4:
+                nc.gpsimd.tensor_tensor(out=g_hi[:, 1, :], in0=ev_lo[:], in1=tab[:, jb, 1, :], op=ALU.mult)
+
         def finish(i, h):
             b, qk, jb = pairs[i]
             dram = (out_q if qk == 0 else out_k)[b].rearrange("(a p) j -> p a j", p=P)
@@ -306,9 +340,16 @@ def tile_sparseattention_pa_kernel(tc, x_bytes, x_scale, wq, bq, wk, bk, out_q, 
                     pending.remove(item)
             if k in (1, 3, 5):
                 table_sincos((k + 1) // 2)
-            products(k)
-            for h in range(2):
-                pending.append((k + 2 if PEADD[k][h] == 0 else k + 1, k, h))
+            if k == GP:
+                gp_evac()
+                pending.append((GP_SLOTS[2] + 2, k, 0))
+                pending.append((GP_SLOTS[4] + 2, k, 1))
+            else:
+                products(k)
+                for h in range(2):
+                    pending.append((k + 2 if PEADD[k][h] == 0 else k + 1, k, h))
+            if k in GP_SLOTS:
+                gp_step(GP_SLOTS.index(k))
 
         kick_ps = psum.tile([P, S], F32, tag="tout", bufs=TOUT_BUFS, name="kick_ps")
         for n in range(KICK):

@@ -40,7 +40,6 @@ def tile_sparseattention_pa_kernel(tc, x_bytes, x_scale, wq, bq, wk, bk, out_q, 
         const = ctx.enter_context(tc.tile_pool(name="const", bufs=1))
         work = ctx.enter_context(tc.tile_pool(name="work", bufs=2))
         psum = ctx.enter_context(tc.psum_pool(name="psum", bufs=4))
-        ctx.enter_context(tc.manual_schedule(engines={mybir.EngineType.PE, mybir.EngineType.Pool}))
 
         idle_rhs = const.tile([P, S], BF16, name="idle_rhs")
         nc.vector.memset(idle_rhs[:], 0.0)
@@ -342,8 +341,8 @@ def tile_sparseattention_pa_kernel(tc, x_bytes, x_scale, wq, bq, wk, bk, out_q, 
                 table_sincos((k + 1) // 2)
             if k == GP:
                 gp_evac()
-                pending.append((GP_SLOTS[2] + 2, k, 0))
-                pending.append((GP_SLOTS[4] + 2, k, 1))
+                pending.append((GP_SLOTS[2] + 3, k, 0))
+                pending.append((GP_SLOTS[4] + 3, k, 1))
             else:
                 products(k)
                 for h in range(2):
@@ -351,6 +350,7 @@ def tile_sparseattention_pa_kernel(tc, x_bytes, x_scale, wq, bq, wk, bk, out_q, 
             if k in GP_SLOTS:
                 gp_step(GP_SLOTS.index(k))
 
+        ctx.enter_context(tc.manual_schedule(engines={mybir.EngineType.PE, mybir.EngineType.Pool}))
         kick_ps = psum.tile([P, S], F32, tag="tout", bufs=TOUT_BUFS, name="kick_ps")
         for n in range(KICK):
             nc.tensor.matmul(out=kick_ps[:], lhsT=idle_rhs[:, 0:P], rhs=idle_rhs[:], start=True, stop=True)

@@ -24,7 +24,7 @@ QSCALE = 128.0 ** -0.5
 PEADD = [(0, 1)] * 15 + [(2, 2)]
 TOUT_BUFS = 4
 ORDER = list(range(16))
-KICK = 5
+KICK = 3
 CH = 256
 FIRST_SLOT = 12
 SLOT_EVERY = 3
@@ -43,11 +43,10 @@ def tile_sparseattention_pa_kernel(tc, x_bytes, x_scale, wq, bq, wk, bk, out_q, 
 
         idle_rhs = const.tile([P, S], BF16, name="idle_rhs")
         nc.vector.memset(idle_rhs[:], 0.0)
-        zrow = const.tile([P, P], F32, name="zrow")
-        nc.vector.memset(zrow[:], 0.0)
 
         sc_bc = const.tile([P, D], F32, name="sc_bc")
-        nc.sync.dma_start(out=zrow[0:8, :], in_=x_scale.rearrange("a b (c p) -> (a b c) p", p=P))
+        sv = const.tile([P, 8], F32, name="sv")
+        nc.sync.dma_start(out=sv[:], in_=x_scale.rearrange("a b (p c) -> (a b p) c", c=8))
         xb = []
         for b in range(2):
             xb_t = const.tile([P, 4 * D], U8, name="xbytes%d" % b)
@@ -81,7 +80,7 @@ def tile_sparseattention_pa_kernel(tc, x_bytes, x_scale, wq, bq, wk, bk, out_q, 
         nc.gpsimd.iota(s_row[:], pattern=[[1, S]], base=0, channel_multiplier=0,
                        allow_small_or_imprecise_dtypes=True)
         ident_b = const.tile([P, P], BF16, name="ident_b")
-        make_identity(nc, ident_b[:])
+        nc.scalar.copy(out=ident_b[:], in_=ident_f[:])
         braw = const.tile([P, P], BF16, name="braw")
         nc.vector.memset(braw[:], 0.0)
         nc.gpsimd.dma_start(out=braw[0:8, :], in_=bq.rearrange("(m p) -> m p", p=P))
@@ -191,10 +190,10 @@ def tile_sparseattention_pa_kernel(tc, x_bytes, x_scale, wq, bq, wk, bk, out_q, 
 
         def x_widen(b, a):
             xw = work.tile([P, D], BF16, tag="xw", bufs=3, name="xw")
-            wd = CH if (b, a) == (0, 0) else D
-            for c0 in range(0, D, wd):
-                nc.vector.tensor_tensor(out=xw[:, c0:c0 + wd], in0=xb[b][:, a * D + c0:a * D + c0 + wd].bitcast(FP8),
-                                        in1=sc_bc[:, c0:c0 + wd], op=ALU.mult)
+            cuts = (0, CH, D) if (b, a) == (0, 0) else (0, D)
+            for (c0, c1) in zip(cuts[0:-1], cuts[1:]):
+                nc.vector.tensor_tensor(out=xw[:, c0:c1], in0=xb[b][:, a * D + c0:a * D + c1].bitcast(FP8),
+                                        in1=sc_bc[:, c0:c1], op=ALU.mult)
             xw_of[(b, a)] = xw
 
         def x_turn(b, a):
@@ -355,16 +354,16 @@ def tile_sparseattention_pa_kernel(tc, x_bytes, x_scale, wq, bq, wk, bk, out_q, 
         for n in range(KICK):
             nc.tensor.matmul(out=kick_ps[:], lhsT=idle_rhs[:, 0:P], rhs=idle_rhs[:], start=True, stop=True)
 
-        sv_ps = psum.tile([P, P], F32, tag="tout", bufs=TOUT_BUFS, name="sv_ps")
-        nc.tensor.transpose(sv_ps[:], zrow[:], ident_f[:])
-        sv = const.tile([P, 8], F32, name="sv")
-        nc.scalar.copy(out=sv[:], in_=sv_ps[:, 0:8])
-        for c0 in range(0, D, CH):
-            sc_ps = psum.tile([P, CH], F32, tag="tout", bufs=TOUT_BUFS, name="sc_ps")
-            for c in range(CH // P):
-                col = c0 // P + c
-                nc.tensor.transpose(sc_ps[:, c * P:(c + 1) * P], sv[:, col:col + 1].to_broadcast([P, P]), ident_f[:])
-            nc.scalar.copy(out=sc_bc[:, c0:c0 + CH], in_=sc_ps[:])
+        sc_ps = []
+        for half in range(2):
+            sc_t = psum.tile([P, 4 * P], F32, tag="tout", bufs=TOUT_BUFS, name="sc_ps")
+            for c in range(4):
+                nc.tensor.transpose(sc_t[:, c * P:(c + 1) * P], sv[:, 4 * half + c:4 * half + c + 1].to_broadcast([P, P]), ident_f[:])
+            sc_ps.append(sc_t)
+        for (n0, n1) in ((0, CH // 8), (CH // 8, P)):
+            for half in range(2):
+                nc.scalar.copy(out=sc_bc[:, 8 * n0:8 * n1].rearrange("p (n c) -> p n c", c=8)[:, :, 4 * half:4 * half + 4],
+                               in_=sc_ps[half][:].rearrange("p (c n) -> p n c", c=4)[:, n0:n1, :])
         x_widen(0, 0)
         x_widen(0, 1)
         due = []

@@ -32,6 +32,7 @@ WORD = [0, 4, 1, 5, 2, 6, 3, 7]
 SHORT_SUMS = 4
 GP = 3
 GP_SLOTS = [4, 6, 8, 10, 12]
+SWAPPED = 8
 
 
 def tile_sparseattention_pa_kernel(tc, x_bytes, x_scale, wq, bq, wk, bk, out_q, out_k):
@@ -368,8 +369,11 @@ def tile_sparseattention_pa_kernel(tc, x_bytes, x_scale, wq, bq, wk, bk, out_q, 
         x_widen(0, 1)
         due = []
         slots_done = 0
-        for n in range(len(seq)):
-            kind, c0, c1 = seq[n]
+        turns = list(seq)
+        for n in range(0, SWAPPED, 2):
+            turns[n], turns[n + 1] = seq[n + 1], seq[n]
+        for n in range(len(turns)):
+            kind, c0, c1 = turns[n]
             if kind == "w":
                 w_turn(c0, c1)
                 if c1 == 1:
@@ -381,11 +385,12 @@ def tile_sparseattention_pa_kernel(tc, x_bytes, x_scale, wq, bq, wk, bk, out_q, 
                     x_widen(nxt // 4, nxt % 4)
                 if c1 == 3:
                     due.append((n + 1, "x", c0))
-            for item in list(due):
-                if item[0] <= n:
-                    quant(item)
-                    due.remove(item)
-            if n == 7:
+            for want in ("x", "w"):
+                for item in list(due):
+                    if item[0] <= n and item[1] == want:
+                        quant(item)
+                        due.remove(item)
+            if n == 8:
                 x_widen(1, 1)
             if n == 3:
                 table_sincos(0)

@@ -29,9 +29,9 @@ CH = 256
 FIRST_SLOT = 12
 SLOT_EVERY = 3
 WORD = [0, 4, 1, 5, 2, 6, 3, 7]
-SHORT_SUMS = 4
-GP = 3
-GP_SLOTS = [4, 6, 8, 10, 12]
+SHORT_SUMS = 16
+GP = -1
+GP_SLOTS = []
 SWAPPED = 8
 
 

@@ -59,9 +59,9 @@ def tile_sparseattention_pa_kernel(tc, x_bytes, x_scale, wq, bq, wk, bk, out_q, 
                 w_raw[(w, h)] = w_t
 
         seq = [("x", 0, 0), ("w", 0, 0), ("x", 0, 1), ("w", 0, 1), ("x", 0, 2), ("w", 1, 0), ("x", 0, 3), ("w", 1, 1),
-               ("w", 2, 0), ("w", 2, 1), ("x", 1, 0), ("w", 3, 0), ("x", 1, 1), ("w", 3, 1), ("x", 1, 2), ("w", 4, 0),
-               ("x", 1, 3), ("w", 4, 1)]
-        for w in (5, 6, 7):
+               ("w", 2, 0), ("w", 2, 1), ("w", 3, 0), ("w", 3, 1), ("x", 1, 0), ("w", 4, 0), ("x", 1, 1), ("w", 4, 1),
+               ("x", 1, 2), ("w", 5, 0), ("x", 1, 3), ("w", 5, 1)]
+        for w in (6, 7):
             seq.append(("w", w, 0))
             seq.append(("w", w, 1))
         seq = [(kind, (WORD[c0] if kind == "w" else c0), c1) for (kind, c0, c1) in seq]
@@ -202,8 +202,11 @@ def tile_sparseattention_pa_kernel(tc, x_bytes, x_scale, wq, bq, wk, bk, out_q, 
             dst = xg[b][:].bitcast(F32).rearrange("p (g r u) -> p g r u", g=2, u=2)[:, :, a * P:(a + 1) * P, :]
             nc.scalar.copy(out=dst, in_=bank[:].rearrange("p (g u r) -> p g r u", g=2, u=2))
 
-        def x_quant(b):
-            nc.vector.quantize_mx(out=xcodes[b][:].bitcast(FP8X4), scales=xscales[b][:], in_=xg[b][:])
+        def x_quant(b, half):
+            for g in range(2):
+                c0 = g * S + half * (S // 2)
+                nc.vector.quantize_mx(out=xcodes[b][:, c0:c0 + S // 2].bitcast(FP8X4), scales=xscales[b][:, c0:c0 + S // 2],
+                                      in_=xg[b][:, 4 * c0:4 * c0 + 2 * S])
 
         wg_of = {}
 
@@ -326,7 +329,7 @@ def tile_sparseattention_pa_kernel(tc, x_bytes, x_scale, wq, bq, wk, bk, out_q, 
             if item[1] == "w":
                 w_quant(item[2])
             else:
-                x_quant(item[2])
+                x_quant(item[2][0], item[2][1])
 
         pending = []
 
@@ -381,16 +384,18 @@ def tile_sparseattention_pa_kernel(tc, x_bytes, x_scale, wq, bq, wk, bk, out_q, 
             else:
                 x_turn(c0, c1)
                 nxt = c0 * 4 + c1 + 2
-                if nxt < 8 and nxt != 5:
+                if nxt < 8 and nxt != 5 and nxt != 4:
                     x_widen(nxt // 4, nxt % 4)
-                if c1 == 3:
-                    due.append((n + 1, "x", c0))
+                if c1 % 2 == 1:
+                    due.append((n + 1, "x", (c0, c1 // 2)))
             for want in ("x", "w"):
                 for item in list(due):
                     if item[0] <= n and item[1] == want:
                         quant(item)
                         due.remove(item)
             if n == 8:
+                x_widen(1, 0)
+            if n == 10:
                 x_widen(1, 1)
             if n == 3:
                 table_sincos(0)

@@ -303,27 +303,55 @@ def tile_sparseattention_pa_kernel(tc, x_bytes, x_scale, wq, bq, wk, bk, out_q, 
             if n == 4:
                 nc.gpsimd.tensor_tensor(out=g_hi[:, 1, :], in0=ev_lo[:], in1=tab[:, jb, 1, :], op=ALU.mult)
 
-        def finish(i, h):
+        def finish(i, h, a0=0, a1=4):
             b, qk, jb = pairs[i]
             dram = (out_q if qk == 0 else out_k)[b].rearrange("(a p) j -> p a j", p=P)
-            bank = psum.tile([P, S], F32, tag="tout", bufs=TOUT_BUFS, name="tout")
-            for a in range(4):
+            bank = psum.tile([P, (a1 - a0) * P], F32, tag="tout", bufs=TOUT_BUFS, name="tout")
+            for a in range(a0, a1):
                 blk = slice(a * P, (a + 1) * P)
+                dst = slice((a - a0) * P, (a - a0 + 1) * P)
                 if h in sum_of[i]:
-                    nc.tensor.transpose(bank[:, blk], sum_of[i][h][:, blk], ident_f[:])
+                    nc.tensor.transpose(bank[:, dst], sum_of[i][h][:, blk], ident_f[:])
                 else:
                     (ta, ka), (tb, kb) = prod_of[i][2 * h], prod_of[i][2 * h + 1]
-                    nc.tensor.matmul(out=bank[:, blk], lhsT=ta[:, ka, blk], rhs=ident_f[:],
+                    nc.tensor.matmul(out=bank[:, dst], lhsT=ta[:, ka, blk], rhs=ident_f[:],
                                      is_transpose=True, start=True, stop=False)
-                    nc.tensor.matmul(out=bank[:, blk], lhsT=tb[:, kb, blk], rhs=ident_f[:],
+                    nc.tensor.matmul(out=bank[:, dst], lhsT=tb[:, kb, blk], rhs=ident_f[:],
                                      is_transpose=True, start=False, stop=True)
-            ost = work.tile([P, S], F32, tag="ost", bufs=8, name="ost")
+            ost = work.tile([P, (a1 - a0) * P], F32, tag="ost", bufs=8, name="ost")
             if qk == 0:
                 nc.scalar.activation(out=ost[:], in_=bank[:], func=ACTF.Copy, scale=QSCALE)
             else:
                 nc.scalar.copy(out=ost[:], in_=bank[:])
             j0 = h * S + jb * P
-            nc.sync.dma_start(out=dram[:, :, j0:j0 + P], in_=ost[:].rearrange("p (a j) -> p a j", a=4))
+            nc.sync.dma_start(out=dram[:, a0:a1, j0:j0 + P], in_=ost[:].rearrange("p (a j) -> p a j", a=a1 - a0))
+
+        def last_pair(i):
+            b, qk, jb = pairs[i]
+            m_lo = work.tile([P, 2, S], F32, tag="m_lo", bufs=4, name="m_lo")
+            m_hi = work.tile([P, 2, S], F32, tag="m_hi", bufs=4, name="m_hi")
+            st = work.tile([P, S], F32, tag="sum0", bufs=3, name="sum0")
+            prod_of[i] = [(m_lo, 0), (m_hi, 1), (m_hi, 0), (m_lo, 1)]
+            sum_of[i] = {}
+            hw = S // 2
+            for c in range(2):
+                cols = slice(c * hw, (c + 1) * hw)
+                for (h, mt) in ((0, m_lo), (1, m_hi)):
+                    col = qk * 8 + 4 * h + jb
+                    nc.vector.scalar_tensor_tensor(out=mt[:, :, cols], in0=acc_of[i][h][:, cols].unsqueeze(1).to_broadcast([P, 2, hw]),
+                                                   scalar=bias[:, col:col + 1], in1=tab[:, jb, :, cols],
+                                                   op0=ALU.add, op1=ALU.mult)
+                finish(i, 1, 2 * c, 2 * c + 2)
+                if c == 0:
+                    for item in list(pending):
+                        finish(item[1], item[2])
+                        pending.remove(item)
+            for c in range(2):
+                cols = slice(c * hw, (c + 1) * hw)
+                nc.vector.tensor_tensor(out=st[:, cols], in0=m_lo[:, 0, cols], in1=m_hi[:, 1, cols], op=ALU.subtract)
+            sum_of[i] = {0: st}
+            for c in range(2):
+                finish(i, 0, 2 * c, 2 * c + 2)
 
         def quant(item):
             if item[1] == "w":
@@ -346,6 +374,8 @@ def tile_sparseattention_pa_kernel(tc, x_bytes, x_scale, wq, bq, wk, bk, out_q, 
                 gp_evac()
                 pending.append((GP_SLOTS[2] + 3, k, 0))
                 pending.append((GP_SLOTS[4] + 3, k, 1))
+            elif k == 15:
+                last_pair(k)
             else:
                 products(k)
                 for h in range(2):

@@ -161,7 +161,7 @@ def tile_sparseattention_pa_kernel(tc, x_bytes, x_scale, wq, bq, wk, bk, out_q, 
         def turn_bias():
             bt_ps = psum.tile([P, P], BF16, tag="tout", bufs=TOUT_BUFS, name="bt_ps")
             nc.tensor.transpose(bt_ps[:], braw[:], ident_b[:])
-            nc.vector.tensor_copy(out=bias[:], in_=bt_ps[:, 0:16])
+            nc.scalar.copy(out=bias[:], in_=bt_ps[:, 0:16])
 
         xg, xcodes, xscales = [], [], []
         for b in range(2):
@@ -203,6 +203,10 @@ def tile_sparseattention_pa_kernel(tc, x_bytes, x_scale, wq, bq, wk, bk, out_q, 
             nc.scalar.copy(out=dst, in_=bank[:].rearrange("p (g u r) -> p g r u", g=2, u=2))
 
         def x_quant(b, half):
+            if b == 1:
+                if half == 1:
+                    nc.vector.quantize_mx(out=xcodes[b][:].bitcast(FP8X4), scales=xscales[b][:], in_=xg[b][:])
+                return
             for g in range(2):
                 c0 = g * S + half * (S // 2)
                 nc.vector.quantize_mx(out=xcodes[b][:, c0:c0 + S // 2].bitcast(FP8X4), scales=xscales[b][:, c0:c0 + S // 2],

@@ -159,7 +159,7 @@ def tile_sparseattention_pa_kernel(tc, x_bytes, x_scale, wq, bq, wk, bk, out_q, 
         bias = const.tile([P, 16], F32, name="bias")
 
         def turn_bias():
-            bt_ps = psum.tile([P, P], BF16, tag="tout", bufs=TOUT_BUFS, name="bt_ps")
+            bt_ps = psum.tile([P, P], BF16, tag="ring", bufs=8, name="bt_ps")
             nc.tensor.transpose(bt_ps[:], braw[:], ident_b[:])
             nc.scalar.copy(out=bias[:], in_=bt_ps[:, 0:16])
 
@@ -180,7 +180,7 @@ def tile_sparseattention_pa_kernel(tc, x_bytes, x_scale, wq, bq, wk, bk, out_q, 
 
         def turn(src_bf16):
             words = src_bf16.bitcast(F32)
-            bank = psum.tile([P, 4 * P], F32, tag="tout", bufs=TOUT_BUFS, name="tin")
+            bank = psum.tile([P, 4 * P], F32, tag="ring", bufs=8, name="tin")
             for g in range(2):
                 for u in range(2):
                     c0 = (2 * g + u) * P
@@ -235,7 +235,7 @@ def tile_sparseattention_pa_kernel(tc, x_bytes, x_scale, wq, bq, wk, bk, out_q, 
             w = qk * 4 + jb
             accs = []
             for h in range(2):
-                acc = psum.tile([P, S], F32, tag="acc", bufs=4, name="acc")
+                acc = psum.tile([P, S], F32, tag="ring", bufs=8, name="acc")
                 for g in range(2):
                     c0 = (2 * h + g) * P
                     nc.tensor.matmul_mx(
@@ -310,7 +310,7 @@ def tile_sparseattention_pa_kernel(tc, x_bytes, x_scale, wq, bq, wk, bk, out_q, 
         def finish(i, h, a0=0, a1=4):
             b, qk, jb = pairs[i]
             dram = (out_q if qk == 0 else out_k)[b].rearrange("(a p) j -> p a j", p=P)
-            bank = psum.tile([P, (a1 - a0) * P], F32, tag="tout", bufs=TOUT_BUFS, name="tout")
+            bank = psum.tile([P, (a1 - a0) * P], F32, tag="ring", bufs=8, name="tout")
             for a in range(a0, a1):
                 blk = slice(a * P, (a + 1) * P)
                 dst = slice((a - a0) * P, (a - a0 + 1) * P)
@@ -388,13 +388,13 @@ def tile_sparseattention_pa_kernel(tc, x_bytes, x_scale, wq, bq, wk, bk, out_q, 
                 gp_step(GP_SLOTS.index(k))
 
         ctx.enter_context(tc.manual_schedule(engines={mybir.EngineType.PE, mybir.EngineType.Pool}))
-        kick_ps = psum.tile([P, S], F32, tag="tout", bufs=TOUT_BUFS, name="kick_ps")
+        kick_ps = psum.tile([P, S], F32, tag="ring", bufs=8, name="kick_ps")
         for n in range(KICK):
             nc.tensor.matmul(out=kick_ps[:], lhsT=idle_rhs[:, 0:P], rhs=idle_rhs[:], start=True, stop=True)
 
         sc_ps = []
         for half in range(2):
-            sc_t = psum.tile([P, 4 * P], F32, tag="tout", bufs=TOUT_BUFS, name="sc_ps")
+            sc_t = psum.tile([P, 4 * P], F32, tag="ring", bufs=8, name="sc_ps")
             for c in range(4):
                 nc.tensor.transpose(sc_t[:, c * P:(c + 1) * P], sv[:, 4 * half + c:4 * half + c + 1].to_broadcast([P, P]), ident_f[:])
             sc_ps.append(sc_t)

@@ -45,6 +45,9 @@ def tile_sparseattention_pa_kernel(tc, x_bytes, x_scale, wq, bq, wk, bk, out_q, 
         idle_rhs = const.tile([P, S], BF16, name="idle_rhs")
         nc.vector.memset(idle_rhs[:], 0.0)
 
+        braw = const.tile([P, P], BF16, name="braw")
+        nc.vector.memset(braw[:], 0.0)
+
         sc_bc = const.tile([P, D], F32, name="sc_bc")
         sv = const.tile([P, 8], F32, name="sv")
         nc.sync.dma_start(out=sv[:], in_=x_scale.rearrange("a b (p c) -> (a b p) c", c=8))
@@ -65,13 +68,16 @@ def tile_sparseattention_pa_kernel(tc, x_bytes, x_scale, wq, bq, wk, bk, out_q, 
             seq.append(("w", w, 0))
             seq.append(("w", w, 1))
         seq = [(kind, (WORD[c0] if kind == "w" else c0), c1) for (kind, c0, c1) in seq]
-        for (kind, c0, c1) in seq:
+        for (n_load, (kind, c0, c1)) in enumerate(seq):
             if kind == "x":
                 nc.sync.dma_start(out=xb[c0][:, c1 * D:(c1 + 1) * D], in_=x_bytes[c0, c1 * P:(c1 + 1) * P, :])
             else:
                 src = wq if c0 < 4 else wk
                 r0 = c1 * S + (c0 % 4) * P
                 nc.sync.dma_start(out=w_raw[(c0, c1)][:], in_=src[r0:r0 + P, :])
+            if n_load == 7:
+                nc.sync.dma_start(out=braw[0:8, :], in_=bq.rearrange("(m p) -> m p", p=P))
+                nc.sync.dma_start(out=braw[8:16, :], in_=bk.rearrange("(m p) -> m p", p=P))
 
         p_i = const.tile([P, 1], I32, name="p_i")
         nc.gpsimd.iota(p_i[:], pattern=[[0, 1]], base=0, channel_multiplier=1)
@@ -82,10 +88,6 @@ def tile_sparseattention_pa_kernel(tc, x_bytes, x_scale, wq, bq, wk, bk, out_q, 
                        allow_small_or_imprecise_dtypes=True)
         ident_b = const.tile([P, P], BF16, name="ident_b")
         nc.scalar.copy(out=ident_b[:], in_=ident_f[:])
-        braw = const.tile([P, P], BF16, name="braw")
-        nc.vector.memset(braw[:], 0.0)
-        nc.gpsimd.dma_start(out=braw[0:8, :], in_=bq.rearrange("(m p) -> m p", p=P))
-        nc.gpsimd.dma_start(out=braw[8:16, :], in_=bk.rearrange("(m p) -> m p", p=P))
 
         zero1 = const.tile([P, 1], F32, name="zero1")
         nc.vector.memset(zero1[:], 0.0)

@@ -408,9 +408,9 @@ def tile_sparseattention_pa_kernel(tc, x_bytes, x_scale, wq, bq, wk, bk, out_q, 
         x_widen(0, 1)
         due = []
         slots_done = 0
-        turns = list(seq)
-        for n in range(0, SWAPPED, 2):
-            turns[n], turns[n + 1] = seq[n + 1], seq[n]
+        xs = [item for item in seq[0:12] if item[0] == "x"]
+        ws = [item for item in seq[0:12] if item[0] == "w"]
+        turns = ws[0:3] + [xs[0], ws[3], xs[1], ws[4], xs[2], ws[5], xs[3], ws[6], ws[7]] + list(seq[12:])
         for n in range(len(turns)):
             kind, c0, c1 = turns[n]
             if kind == "w":
@@ -429,9 +429,9 @@ def tile_sparseattention_pa_kernel(tc, x_bytes, x_scale, wq, bq, wk, bk, out_q, 
                     if item[0] <= n and item[1] == want:
                         quant(item)
                         due.remove(item)
-            if n == 8:
-                x_widen(1, 0)
             if n == 10:
+                x_widen(1, 0)
+            if n == 11:
                 x_widen(1, 1)
             if n == 3:
                 table_sincos(0)

@@ -26,7 +26,7 @@ TOUT_BUFS = 4
 ORDER = list(range(16))
 KICK = 3
 CH = 256
-FIRST_SLOT = 12
+FIRST_SLOT = 14
 SLOT_EVERY = 3
 WORD = [0, 4, 1, 5, 2, 6, 3, 7]
 SHORT_SUMS = 16
@@ -410,7 +410,10 @@ def tile_sparseattention_pa_kernel(tc, x_bytes, x_scale, wq, bq, wk, bk, out_q, 
         slots_done = 0
         xs = [item for item in seq[0:12] if item[0] == "x"]
         ws = [item for item in seq[0:12] if item[0] == "w"]
-        turns = ws[0:3] + [xs[0], ws[3], xs[1], ws[4], xs[2], ws[5], xs[3], ws[6], ws[7]] + list(seq[12:])
+        xs2 = [item for item in seq[12:] if item[0] == "x"]
+        ws2 = [item for item in seq[12:] if item[0] == "w"]
+        turns = ws[0:3] + [xs[0], ws[3], xs[1], ws[4], xs[2], ws[5], xs[3], ws[6], ws[7]]
+        turns = turns + ws2[0:2] + [xs2[0], ws2[2], xs2[1], ws2[3], xs2[2], ws2[4], xs2[3], ws2[5], ws2[6], ws2[7]]
         for n in range(len(turns)):
             kind, c0, c1 = turns[n]
             if kind == "w":

@@ -26,7 +26,7 @@ TOUT_BUFS = 4
 ORDER = list(range(16))
 KICK = 3
 CH = 256
-FIRST_SLOT = 14
+FIRST_SLOT = 15
 SLOT_EVERY = 3
 WORD = [0, 4, 1, 5, 2, 6, 3, 7]
 SHORT_SUMS = 16
@@ -68,6 +68,10 @@ def tile_sparseattention_pa_kernel(tc, x_bytes, x_scale, wq, bq, wk, bk, out_q, 
             seq.append(("w", w, 0))
             seq.append(("w", w, 1))
         seq = [(kind, (WORD[c0] if kind == "w" else c0), c1) for (kind, c0, c1) in seq]
+        late_x = [item for item in seq[12:] if item[0] == "x"]
+        late_w = [item for item in seq[12:] if item[0] == "w"]
+        late = late_w[0:3] + [late_x[0], late_w[3], late_x[1], late_w[4], late_x[2], late_w[5], late_x[3], late_w[6], late_w[7]]
+        seq = seq[0:6] + [seq[7], seq[6]] + seq[8:12] + late
         for (n_load, (kind, c0, c1)) in enumerate(seq):
             if kind == "x":
                 nc.sync.dma_start(out=xb[c0][:, c1 * D:(c1 + 1) * D], in_=x_bytes[c0, c1 * P:(c1 + 1) * P, :])
@@ -410,10 +414,7 @@ def tile_sparseattention_pa_kernel(tc, x_bytes, x_scale, wq, bq, wk, bk, out_q, 
         slots_done = 0
         xs = [item for item in seq[0:12] if item[0] == "x"]
         ws = [item for item in seq[0:12] if item[0] == "w"]
-        xs2 = [item for item in seq[12:] if item[0] == "x"]
-        ws2 = [item for item in seq[12:] if item[0] == "w"]
-        turns = ws[0:3] + [xs[0], ws[3], xs[1], ws[4], xs[2], ws[5], xs[3], ws[6], ws[7]]
-        turns = turns + ws2[0:2] + [xs2[0], ws2[2], xs2[1], ws2[3], xs2[2], ws2[4], xs2[3], ws2[5], ws2[6], ws2[7]]
+        turns = ws[0:4] + [xs[0], ws[4], xs[1], ws[5], xs[2], ws[6], xs[3], ws[7]] + late
         for n in range(len(turns)):
             kind, c0, c1 = turns[n]
             if kind == "w":
@@ -432,9 +433,9 @@ def tile_sparseattention_pa_kernel(tc, x_bytes, x_scale, wq, bq, wk, bk, out_q, 
                     if item[0] <= n and item[1] == want:
                         quant(item)
                         due.remove(item)
-            if n == 10:
-                x_widen(1, 0)
             if n == 11:
+                x_widen(1, 0)
+            if n == 12:
                 x_widen(1, 1)
             if n == 3:
                 table_sincos(0)

@@ -178,9 +178,9 @@ def tile_sparseattention_pa_kernel(tc, x_bytes, x_scale, wq, bq, wk, bk, out_q, 
             xcodes.append(xc_t)
             xscales.append(xs_t)
         wcodes, wscales = [], []
-        for w in range(8):
-            wc_t = const.tile([P, 4 * P], U32, name="wcodes%d" % w, align_bytes=64)
-            ws_t = const.tile([P, 4 * P], U8, name="wscales%d" % w, align_bytes=64)
+        for w in range(4):
+            wc_t = const.tile([P, 8 * P], U32, name="wcodes%d" % w, align_bytes=64)
+            ws_t = const.tile([P, 8 * P], U8, name="wscales%d" % w, align_bytes=64)
             wcodes.append(wc_t)
             wscales.append(ws_t)
 
@@ -221,11 +221,12 @@ def tile_sparseattention_pa_kernel(tc, x_bytes, x_scale, wq, bq, wk, bk, out_q, 
         wg_of = {}
 
         def w_turn(w, h):
-            if h == 0:
-                wg_new = work.tile([P, 2 * D], BF16, tag="wg", bufs=3, name="wg", align_bytes=64)
+            if h == 0 and w < 4:
+                wg_new = work.tile([P, 4 * D], BF16, tag="wg", bufs=3, name="wg", align_bytes=64)
                 wg_of[w] = wg_new
             bank = turn(w_raw[(w, h)][:])
-            nc.scalar.copy(out=wg_of[w][:, h * D:(h + 1) * D].bitcast(F32).rearrange("p (g r u) -> p g r u", g=2, u=2),
+            part = 2 * (w // 4) + h
+            nc.scalar.copy(out=wg_of[w % 4][:, part * D:(part + 1) * D].bitcast(F32).rearrange("p (g r u) -> p g r u", g=2, u=2),
                            in_=bank[:].rearrange("p (g u r) -> p g r u", g=2, u=2))
 
         def w_quant(w):
@@ -243,11 +244,11 @@ def tile_sparseattention_pa_kernel(tc, x_bytes, x_scale, wq, bq, wk, bk, out_q, 
             for h in range(2):
                 acc = psum.tile([P, S], F32, tag="ring", bufs=8, name="acc")
                 for g in range(2):
-                    c0 = (2 * h + g) * P
+                    c0 = (4 * qk + 2 * h + g) * P
                     nc.tensor.matmul_mx(
                         out=acc[:],
-                        lhsT=wcodes[w][:, c0:c0 + P].bitcast(FP8X4),
-                        lhsT_scale=wscales[w][:, c0:c0 + P],
+                        lhsT=wcodes[jb][:, c0:c0 + P].bitcast(FP8X4),
+                        lhsT_scale=wscales[jb][:, c0:c0 + P],
                         rhs=xcodes[b][:, g * S:(g + 1) * S].bitcast(FP8X4),
                         rhs_scale=xscales[b][:, g * S:(g + 1) * S],
                         start=(g == 0), stop=(g == 1),
@@ -419,8 +420,8 @@ def tile_sparseattention_pa_kernel(tc, x_bytes, x_scale, wq, bq, wk, bk, out_q, 
             kind, c0, c1 = turns[n]
             if kind == "w":
                 w_turn(c0, c1)
-                if c1 == 1:
-                    due.append((n + 2, "w", c0))
+                if c1 == 1 and c0 >= 4:
+                    due.append((n + 2, "w", c0 % 4))
             else:
                 x_turn(c0, c1)
                 nxt = c0 * 4 + c1 + 2

@@ -24,7 +24,7 @@ QSCALE = 128.0 ** -0.5
 PEADD = [(0, 1)] * 15 + [(2, 2)]
 TOUT_BUFS = 4
 ORDER = list(range(16))
-KICK = 3
+KICK = 0
 CH = 256
 FIRST_SLOT = 15
 SLOT_EVERY = 3
@@ -395,7 +395,7 @@ def tile_sparseattention_pa_kernel(tc, x_bytes, x_scale, wq, bq, wk, bk, out_q, 
                 gp_step(GP_SLOTS.index(k))
 
         ctx.enter_context(tc.manual_schedule(engines={mybir.EngineType.PE, mybir.EngineType.Pool}))
-        kick_ps = psum.tile([P, S], F32, tag="ring", bufs=8, name="kick_ps")
+        kick_ps = idle_rhs
         for n in range(KICK):
             nc.tensor.matmul(out=kick_ps[:], lhsT=idle_rhs[:, 0:P], rhs=idle_rhs[:], start=True, stop=True)
 

from contextlib import ExitStack

import concourse.mybir as mybir
from concourse.masks import make_identity

FLOPS = 2 * 1024 * 1024 * 2048

F32 = mybir.dt.float32
BF16 = mybir.dt.bfloat16
U8 = mybir.dt.uint8
U32 = mybir.dt.uint32
I32 = mybir.dt.int32
FP8 = mybir.dt.float8_e4m3fn
FP8X4 = mybir.dt.float8_e4m3fn_x4
ALU = mybir.AluOpType
ACTF = mybir.ActivationFunctionType

P = 128
S = 512
D = 1024
PI = 3.141592653589793
RHO = 10000.0 ** (-1.0 / 512.0)
QSCALE = 128.0 ** -0.5
PEADD = [(0, 1)] * 15 + [(2, 2)]
TOUT_BUFS = 4
ORDER = list(range(16))
KICK = 0
CH = 256
FIRST_SLOT = 15
SLOT_EVERY = 3
WORD = [0, 4, 1, 5, 2, 6, 3, 7]
SHORT_SUMS = 16
GP = -1
GP_SLOTS = []
SWAPPED = 8


def tile_sparseattention_pa_kernel(tc, x_bytes, x_scale, wq, bq, wk, bk, out_q, out_k):
    nc = tc.nc
    with ExitStack() as ctx:
        const = ctx.enter_context(tc.tile_pool(name="const", bufs=1))
        work = ctx.enter_context(tc.tile_pool(name="work", bufs=2))
        psum = ctx.enter_context(tc.psum_pool(name="psum", bufs=4))

        idle_rhs = const.tile([P, S], BF16, name="idle_rhs")
        nc.vector.memset(idle_rhs[:], 0.0)

        braw = const.tile([P, P], BF16, name="braw")
        nc.vector.memset(braw[:], 0.0)

        sc_bc = const.tile([P, D], F32, name="sc_bc")
        sv = const.tile([P, 8], F32, name="sv")
        nc.sync.dma_start(out=sv[:], in_=x_scale.rearrange("a b (p c) -> (a b p) c", c=8))
        xb = []
        for b in range(2):
            xb_t = const.tile([P, 4 * D], U8, name="xbytes%d" % b)
            xb.append(xb_t)
        w_raw = {}
        for w in range(8):
            for h in range(2):
                w_t = const.tile([P, D], BF16, name="wraw%d_%d" % (w, h))
                w_raw[(w, h)] = w_t

        seq = [("x", 0, 0), ("w", 0, 0), ("x", 0, 1), ("w", 0, 1), ("x", 0, 2), ("w", 1, 0), ("x", 0, 3), ("w", 1, 1),
               ("w", 2, 0), ("w", 2, 1), ("w", 3, 0), ("w", 3, 1), ("x", 1, 0), ("w", 4, 0), ("x", 1, 1), ("w", 4, 1),
               ("x", 1, 2), ("w", 5, 0), ("x", 1, 3), ("w", 5, 1)]
        for w in (6, 7):
            seq.append(("w", w, 0))
            seq.append(("w", w, 1))
        seq = [(kind, (WORD[c0] if kind == "w" else c0), c1) for (kind, c0, c1) in seq]
        late_x = [item for item in seq[12:] if item[0] == "x"]
        late_w = [item for item in seq[12:] if item[0] == "w"]
        late = late_w[0:3] + [late_x[0], late_w[3], late_x[1], late_w[4], late_x[2], late_w[5], late_x[3], late_w[6], late_w[7]]
        seq = seq[0:6] + [seq[7], seq[6]] + seq[8:12] + late
        for (n_load, (kind, c0, c1)) in enumerate(seq):
            if kind == "x":
                nc.sync.dma_start(out=xb[c0][:, c1 * D:(c1 + 1) * D], in_=x_bytes[c0, c1 * P:(c1 + 1) * P, :])
            else:
                src = wq if c0 < 4 else wk
                r0 = c1 * S + (c0 % 4) * P
                nc.sync.dma_start(out=w_raw[(c0, c1)][:], in_=src[r0:r0 + P, :])
            if n_load == 7:
                nc.sync.dma_start(out=braw[0:8, :], in_=bq.rearrange("(m p) -> m p", p=P))
                nc.sync.dma_start(out=braw[8:16, :], in_=bk.rearrange("(m p) -> m p", p=P))

        p_i = const.tile([P, 1], I32, name="p_i")
        nc.gpsimd.iota(p_i[:], pattern=[[0, 1]], base=0, channel_multiplier=1)
        ident_f = const.tile([P, P], F32, name="ident_f")
        make_identity(nc, ident_f[:])
        s_row = const.tile([P, S], F32, name="s_row")
        nc.gpsimd.iota(s_row[:], pattern=[[1, S]], base=0, channel_multiplier=0,
                       allow_small_or_imprecise_dtypes=True)
        ident_b = const.tile([P, P], BF16, name="ident_b")
        nc.scalar.copy(out=ident_b[:], in_=ident_f[:])

        zero1 = const.tile([P, 1], F32, name="zero1")
        nc.vector.memset(zero1[:], 0.0)
        junk = const.tile([P, 1], F32, name="junk")
        nc.scalar.activation(out=junk[:], in_=zero1[:], func=ACTF.Sin)

        bits = const.tile([P, 8], I32, name="bits")
        fac = const.tile([P, 8], F32, name="fac")
        for k in range(7):
            nc.vector.tensor_scalar(out=bits[:, k:k + 1], in0=p_i[:], scalar1=k, scalar2=1,
                                    op0=ALU.logical_shift_right, op1=ALU.bitwise_and)
        for k in range(7):
            nc.vector.tensor_scalar(out=fac[:, k:k + 1], in0=bits[:, k:k + 1],
                                    scalar1=RHO ** (2 ** k) - 1.0, scalar2=1.0,
                                    op0=ALU.mult, op1=ALU.add)
        nc.vector.tensor_scalar(out=fac[:, 7:8], in0=bits[:, 0:1], scalar1=0.0,
                                scalar2=1.0 / (2.0 * PI), op0=ALU.mult, op1=ALU.add)
        f4 = const.tile([P, 4], F32, name="f4")
        nc.vector.tensor_tensor(out=f4[:], in0=fac[:, 0:4], in1=fac[:, 4:8], op=ALU.mult)
        f2 = const.tile([P, 2], F32, name="f2")
        nc.vector.tensor_tensor(out=f2[:], in0=f4[:, 0:2], in1=f4[:, 2:4], op=ALU.mult)
        f1 = const.tile([P, 1], F32, name="f1")
        nc.vector.tensor_tensor(out=f1[:], in0=f2[:, 0:1], in1=f2[:, 1:2], op=ALU.mult)
        g4 = const.tile([P, 4], F32, name="g4")
        for jb in range(2):
            nc.vector.tensor_scalar(out=g4[:, jb:jb + 1], in0=f1[:], scalar1=RHO ** (128 * jb),
                                    scalar2=None, op0=ALU.mult)
        th2 = const.tile([P, 2], F32, name="th2")
        nc.vector.tensor_scalar(out=th2[:, 0:1], in0=f1[:], scalar1=RHO ** 256 * 2.0 * PI, scalar2=None, op0=ALU.mult)
        nc.vector.tensor_scalar(out=th2[:, 1:2], in0=f1[:], scalar1=-(RHO ** 256) * 2.0 * PI, scalar2=None, op0=ALU.mult)
        th3 = const.tile([P, 2], F32, name="th3")
        nc.vector.tensor_scalar(out=th3[:, 0:1], in0=f1[:], scalar1=RHO ** 384 * 2.0 * PI, scalar2=None, op0=ALU.mult)
        nc.vector.tensor_scalar(out=th3[:, 1:2], in0=f1[:], scalar1=-(RHO ** 384) * 2.0 * PI, scalar2=None, op0=ALU.mult)

        tab = const.tile([P, 4, 2, S], F32, name="tab")
        d_all = const.tile([P, 2 * S], F32, name="d_all")

        def table_turns(jb):
            cols = slice(jb * S, (jb + 1) * S)
            n_t = work.tile([P, S], I32, tag="n_t", name="n_t")
            nc.vector.tensor_scalar(out=n_t[:], in0=s_row[:], scalar1=g4[:, jb:jb + 1], scalar2=0.0,
                                    op0=ALU.mult, op1=ALU.add)
            nc.vector.scalar_tensor_tensor(out=d_all[:, cols], in0=s_row[:], scalar=g4[:, jb:jb + 1], in1=n_t[:],
                                           op0=ALU.mult, op1=ALU.subtract)

        table_turns(0)
        table_turns(1)

        def table_sincos(jb):
            if jb == 3:
                nc.scalar.activation(out=tab[:, 3, 1, :], in_=s_row[:], func=ACTF.Sin, scale=th3[:, 0:1])
                nc.scalar.activation(out=tab[:, 3, 0, :], in_=s_row[:], func=ACTF.Sin, scale=th3[:, 1:2], bias=0.5 * PI)
                return
            if jb == 2:
                fh = slice(0, S // 2)
                sh = slice(S // 2, S)
                plus, minus = th2[:, 0:1], th2[:, 1:2]
                nc.scalar.activation(out=tab[:, 2, 1, fh], in_=s_row[:, fh], func=ACTF.Sin, scale=plus)
                nc.scalar.activation(out=tab[:, 2, 1, sh], in_=s_row[:, sh], func=ACTF.Sin, scale=minus, bias=PI)
                nc.scalar.activation(out=tab[:, 2, 0, fh], in_=s_row[:, fh], func=ACTF.Sin, scale=minus, bias=0.5 * PI)
                a_h = work.tile([P, S // 2], F32, tag="a_h", name="a_h")
                nc.scalar.activation(out=a_h[:], in_=s_row[:, sh], func=ACTF.Abs, scale=plus, bias=-PI)
                nc.scalar.activation(out=tab[:, 2, 0, sh], in_=a_h[:], func=ACTF.Sin, bias=-0.5 * PI)
                return
            cols = slice(jb * S, (jb + 1) * S)
            nc.scalar.activation(out=tab[:, jb, 1, :], in_=d_all[:, cols], func=ACTF.Sin, scale=2.0 * PI)
            a_t = work.tile([P, S], F32, tag="a_t", name="a_t")
            nc.scalar.activation(out=a_t[:], in_=d_all[:, cols], func=ACTF.Abs)
            nc.scalar.activation(out=tab[:, jb, 0, :], in_=a_t[:], func=ACTF.Sin, scale=-2.0 * PI, bias=0.5 * PI)

        bias = const.tile([P, 16], F32, name="bias")

        def turn_bias():
            bt_ps = psum.tile([P, P], BF16, tag="ring", bufs=8, name="bt_ps")
            nc.tensor.transpose(bt_ps[:], braw[:], ident_b[:])
            nc.scalar.copy(out=bias[:], in_=bt_ps[:, 0:16])

        xg, xcodes, xscales = [], [], []
        for b in range(2):
            xg_t = const.tile([P, 2 * S * 4], BF16, name="xg%d" % b, align_bytes=64)
            xc_t = const.tile([P, 2 * S], U32, name="xcodes%d" % b, align_bytes=64)
            xs_t = const.tile([P, 2 * S], U8, name="xscales%d" % b, align_bytes=64)
            xg.append(xg_t)
            xcodes.append(xc_t)
            xscales.append(xs_t)
        wcodes, wscales = [], []
        for w in range(4):
            wc_t = const.tile([P, 8 * P], U32, name="wcodes%d" % w, align_bytes=64)
            ws_t = const.tile([P, 8 * P], U8, name="wscales%d" % w, align_bytes=64)
            wcodes.append(wc_t)
            wscales.append(ws_t)

        def turn(src_bf16):
            words = src_bf16.bitcast(F32)
            bank = psum.tile([P, 4 * P], F32, tag="ring", bufs=8, name="tin")
            for g in range(2):
                for u in range(2):
                    c0 = (2 * g + u) * P
                    nc.tensor.transpose(bank[:, c0:c0 + P], words[:, 256 * g + u:256 * (g + 1):2], ident_f[:])
            return bank

        xw_of = {}

        def x_widen(b, a):
            xw = work.tile([P, D], BF16, tag="xw", bufs=3, name="xw")
            cuts = (0, CH, D) if (b, a) == (0, 0) else (0, D)
            for (c0, c1) in zip(cuts[0:-1], cuts[1:]):
                nc.vector.tensor_tensor(out=xw[:, c0:c1], in0=xb[b][:, a * D + c0:a * D + c1].bitcast(FP8),
                                        in1=sc_bc[:, c0:c1], op=ALU.mult)
            xw_of[(b, a)] = xw

        def x_turn(b, a):
            bank = turn(xw_of[(b, a)][:])
            dst = xg[b][:].bitcast(F32).rearrange("p (g r u) -> p g r u", g=2, u=2)[:, :, a * P:(a + 1) * P, :]
            nc.scalar.copy(out=dst, in_=bank[:].rearrange("p (g u r) -> p g r u", g=2, u=2))

        def x_quant(b, half):
            if b == 1:
                if half == 1:
                    nc.vector.quantize_mx(out=xcodes[b][:].bitcast(FP8X4), scales=xscales[b][:], in_=xg[b][:])
                return
            for g in range(2):
                c0 = g * S + half * (S // 2)
                nc.vector.quantize_mx(out=xcodes[b][:, c0:c0 + S // 2].bitcast(FP8X4), scales=xscales[b][:, c0:c0 + S // 2],
                                      in_=xg[b][:, 4 * c0:4 * c0 + 2 * S])

        wg_of = {}

        def w_turn(w, h):
            if h == 0 and w < 4:
                wg_new = work.tile([P, 4 * D], BF16, tag="wg", bufs=3, name="wg", align_bytes=64)
                wg_of[w] = wg_new
            bank = turn(w_raw[(w, h)][:])
            part = 2 * (w // 4) + h
            nc.scalar.copy(out=wg_of[w % 4][:, part * D:(part + 1) * D].bitcast(F32).rearrange("p (g r u) -> p g r u", g=2, u=2),
                           in_=bank[:].rearrange("p (g u r) -> p g r u", g=2, u=2))

        def w_quant(w):
            nc.vector.quantize_mx(out=wcodes[w][:].bitcast(FP8X4), scales=wscales[w][:], in_=wg_of[w][:])

        pairs = [(b, qk, jb) for b in range(2) for jb in range(4) for qk in range(2)]
        acc_of = {}
        prod_of = {}
        sum_of = {}

        def mx(i):
            b, qk, jb = pairs[i]
            w = qk * 4 + jb
            accs = []
            for h in range(2):
                acc = psum.tile([P, S], F32, tag="ring", bufs=8, name="acc")
                for g in range(2):
                    c0 = (4 * qk + 2 * h + g) * P
                    nc.tensor.matmul_mx(
                        out=acc[:],
                        lhsT=wcodes[jb][:, c0:c0 + P].bitcast(FP8X4),
                        lhsT_scale=wscales[jb][:, c0:c0 + P],
                        rhs=xcodes[b][:, g * S:(g + 1) * S].bitcast(FP8X4),
                        rhs_scale=xscales[b][:, g * S:(g + 1) * S],
                        start=(g == 0), stop=(g == 1),
                    )
                accs.append(acc)
            acc_of[i] = accs

        def pe_adds(i, h):
            return PEADD[i][h] == 1

        def products(i):
            b, qk, jb = pairs[i]
            m_lo = work.tile([P, 2, S], F32, tag="m_lo", bufs=4, name="m_lo")
            m_hi = work.tile([P, 2, S], F32, tag="m_hi", bufs=4, name="m_hi")
            for (h, mt) in ((0, m_lo), (1, m_hi)):
                c = qk * 8 + 4 * h + jb
                nc.vector.scalar_tensor_tensor(out=mt[:], in0=acc_of[i][h][:].unsqueeze(1).to_broadcast([P, 2, S]),
                                               scalar=bias[:, c:c + 1], in1=tab[:, jb, :, :],
                                               op0=ALU.add, op1=ALU.mult)
            prod_of[i] = [(m_lo, 0), (m_hi, 1), (m_hi, 0), (m_lo, 1)]
            res = {}
            for h in range(2):
                if not pe_adds(i, h):
                    st = work.tile([P, S], F32, tag="sum%d" % h, bufs=3, name="sum%d" % h)
                    (ta, ka), (tb, kb) = prod_of[i][2 * h], prod_of[i][2 * h + 1]
                    adder = nc.vector if PEADD[i][h] == 2 else nc.gpsimd
                    wd = P if (PEADD[i][h] == 0 and i < SHORT_SUMS) else S
                    for c0 in range(0, S, wd):
                        adder.tensor_tensor(out=st[:, c0:c0 + wd], in0=ta[:, ka, c0:c0 + wd], in1=tb[:, kb, c0:c0 + wd],
                                            op=(ALU.subtract if h == 0 else ALU.add))
                    res[h] = st
            sum_of[i] = res

        gp_tiles = {}

        def gp_evac():
            b, qk, jb = pairs[GP]
            for h in range(2):
                ev = const.tile([P, S], F32, name="gp_ev%d" % h)
                c = qk * 8 + 4 * h + jb
                nc.scalar.activation(out=ev[:], in_=acc_of[GP][h][:], func=ACTF.Identity, bias=bias[:, c:c + 1])
                gp_tiles["ev%d" % h] = ev
            g_lo = const.tile([P, 2, S], F32, name="gp_lo")
            g_hi = const.tile([P, 2, S], F32, name="gp_hi")
            g_st = const.tile([P, S], F32, name="gp_st")
            gp_tiles["lo"] = g_lo
            gp_tiles["hi"] = g_hi
            prod_of[GP] = [(g_lo, 0), (g_lo, 1), (g_hi, 0), (g_hi, 1)]
            sum_of[GP] = {0: g_st}

        def gp_step(n):
            b, qk, jb = pairs[GP]
            ev_lo, ev_hi = gp_tiles["ev0"], gp_tiles["ev1"]
            g_lo, g_hi = gp_tiles["lo"], gp_tiles["hi"]
            if n == 0:
                nc.gpsimd.tensor_tensor(out=g_lo[:, 0, :], in0=ev_lo[:], in1=tab[:, jb, 0, :], op=ALU.mult)
            if n == 1:
                nc.gpsimd.tensor_tensor(out=g_lo[:, 1, :], in0=ev_hi[:], in1=tab[:, jb, 1, :], op=ALU.mult)
            if n == 2:
                nc.gpsimd.tensor_tensor(out=sum_of[GP][0][:], in0=g_lo[:, 0, :], in1=g_lo[:, 1, :], op=ALU.subtract)
            if n == 3:
                nc.gpsimd.tensor_tensor(out=g_hi[:, 0, :], in0=ev_hi[:], in1=tab[:, jb, 0, :], op=ALU.mult)
            if n == 4:
                nc.gpsimd.tensor_tensor(out=g_hi[:, 1, :], in0=ev_lo[:], in1=tab[:, jb, 1, :], op=ALU.mult)

        def finish(i, h, a0=0, a1=4):
            b, qk, jb = pairs[i]
            dram = (out_q if qk == 0 else out_k)[b].rearrange("(a p) j -> p a j", p=P)
            bank = psum.tile([P, (a1 - a0) * P], F32, tag="ring", bufs=8, name="tout")
            for a in range(a0, a1):
                blk = slice(a * P, (a + 1) * P)
                dst = slice((a - a0) * P, (a - a0 + 1) * P)
                if h in sum_of[i]:
                    nc.tensor.transpose(bank[:, dst], sum_of[i][h][:, blk], ident_f[:])
                else:
                    (ta, ka), (tb, kb) = prod_of[i][2 * h], prod_of[i][2 * h + 1]
                    nc.tensor.matmul(out=bank[:, dst], lhsT=ta[:, ka, blk], rhs=ident_f[:],
                                     is_transpose=True, start=True, stop=False)
                    nc.tensor.matmul(out=bank[:, dst], lhsT=tb[:, kb, blk], rhs=ident_f[:],
                                     is_transpose=True, start=False, stop=True)
            ost = work.tile([P, (a1 - a0) * P], F32, tag="ost", bufs=8, name="ost")
            if qk == 0:
                nc.scalar.activation(out=ost[:], in_=bank[:], func=ACTF.Copy, scale=QSCALE)
            else:
                nc.scalar.copy(out=ost[:], in_=bank[:])
            j0 = h * S + jb * P
            nc.sync.dma_start(out=dram[:, a0:a1, j0:j0 + P], in_=ost[:].rearrange("p (a j) -> p a j", a=a1 - a0))

        def last_pair(i):
            b, qk, jb = pairs[i]
            m_lo = work.tile([P, 2, S], F32, tag="m_lo", bufs=4, name="m_lo")
            m_hi = work.tile([P, 2, S], F32, tag="m_hi", bufs=4, name="m_hi")
            st = work.tile([P, S], F32, tag="sum0", bufs=3, name="sum0")
            prod_of[i] = [(m_lo, 0), (m_hi, 1), (m_hi, 0), (m_lo, 1)]
            sum_of[i] = {}
            hw = S // 2
            for c in range(2):
                cols = slice(c * hw, (c + 1) * hw)
                for (h, mt) in ((0, m_lo), (1, m_hi)):
                    col = qk * 8 + 4 * h + jb
                    nc.vector.scalar_tensor_tensor(out=mt[:, :, cols], in0=acc_of[i][h][:, cols].unsqueeze(1).to_broadcast([P, 2, hw]),
                                                   scalar=bias[:, col:col + 1], in1=tab[:, jb, :, cols],
                                                   op0=ALU.add, op1=ALU.mult)
                finish(i, 1, 2 * c, 2 * c + 2)
                if c == 0:
                    for item in list(pending):
                        finish(item[1], item[2])
                        pending.remove(item)
            for c in range(2):
                cols = slice(c * hw, (c + 1) * hw)
                nc.vector.tensor_tensor(out=st[:, cols], in0=m_lo[:, 0, cols], in1=m_hi[:, 1, cols], op=ALU.subtract)
            sum_of[i] = {0: st}
            for c in range(2):
                finish(i, 0, 2 * c, 2 * c + 2)

        def quant(item):
            if item[1] == "w":
                w_quant(item[2])
            else:
                x_quant(item[2][0], item[2][1])

        pending = []

        def slot(k):
            if k + 1 < 16:
                mx(k + 1)
            for item in list(pending):
                if item[0] <= k:
                    finish(item[1], item[2])
                    pending.remove(item)
            if k in (1, 3, 5):
                table_sincos((k + 1) // 2)
            if k == GP:
                gp_evac()
                pending.append((GP_SLOTS[2] + 3, k, 0))
                pending.append((GP_SLOTS[4] + 3, k, 1))
            elif k == 15:
                last_pair(k)
            else:
                products(k)
                for h in range(2):
                    pending.append((k + 2 if PEADD[k][h] == 0 else k + 1, k, h))
            if k in GP_SLOTS:
                gp_step(GP_SLOTS.index(k))

        ctx.enter_context(tc.manual_schedule(engines={mybir.EngineType.PE, mybir.EngineType.Pool}))
        kick_ps = idle_rhs
        for n in range(KICK):
            nc.tensor.matmul(out=kick_ps[:], lhsT=idle_rhs[:, 0:P], rhs=idle_rhs[:], start=True, stop=True)

        sc_ps = []
        for half in range(2):
            sc_t = psum.tile([P, 4 * P], F32, tag="ring", bufs=8, name="sc_ps")
            for c in range(4):
                nc.tensor.transpose(sc_t[:, c * P:(c + 1) * P], sv[:, 4 * half + c:4 * half + c + 1].to_broadcast([P, P]), ident_f[:])
            sc_ps.append(sc_t)
        for (n0, n1) in ((0, CH // 8), (CH // 8, P)):
            for half in range(2):
                nc.scalar.copy(out=sc_bc[:, 8 * n0:8 * n1].rearrange("p (n c) -> p n c", c=8)[:, :, 4 * half:4 * half + 4],
                               in_=sc_ps[half][:].rearrange("p (c n) -> p n c", c=4)[:, n0:n1, :])
        x_widen(0, 0)
        x_widen(0, 1)
        due = []
        slots_done = 0
        xs = [item for item in seq[0:12] if item[0] == "x"]
        ws = [item for item in seq[0:12] if item[0] == "w"]
        turns = ws[0:4] + [xs[0], ws[4], xs[1], ws[5], xs[2], ws[6], xs[3], ws[7]] + late
        for n in range(len(turns)):
            kind, c0, c1 = turns[n]
            if kind == "w":
                w_turn(c0, c1)
                if c1 == 1 and c0 >= 4:
                    due.append((n + 2, "w", c0 % 4))
            else:
                x_turn(c0, c1)
                nxt = c0 * 4 + c1 + 2
                if nxt < 8 and nxt != 5 and nxt != 4:
                    x_widen(nxt // 4, nxt % 4)
                if c1 % 2 == 1:
                    due.append((n + 1, "x", (c0, c1 // 2)))
            for want in ("x", "w"):
                for item in list(due):
                    if item[0] <= n and item[1] == want:
                        quant(item)
                        due.remove(item)
            if n == 11:
                x_widen(1, 0)
            if n == 12:
                x_widen(1, 1)
            if n == 3:
                table_sincos(0)
            if n == 10:
                turn_bias()
            if n == FIRST_SLOT - 1:
                mx(0)
            if n >= FIRST_SLOT and (n - FIRST_SLOT) % SLOT_EVERY == 0:
                slot(slots_done)
                slots_done = slots_done + 1
        for item in due:
            quant(item)
        for k in range(slots_done, 16):
            slot(k)
        for item in pending:
            finish(item[1], item[2])
